import numpy as np
import ml_dtypes


def mxq(x, axis, fmt="e4m3"):
    dtype, down = {"e4m3": (ml_dtypes.float8_e4m3fn, 7), "e5m2": (ml_dtypes.float8_e5m2, 14)}[fmt]
    v = np.moveaxis(np.asarray(x, np.float32).astype(ml_dtypes.bfloat16).astype(np.float64), axis, -1)
    blocks = v.reshape(v.shape[:-1] + (-1, 32))
    amax = np.abs(blocks).max(-1, keepdims=True)
    byte = np.maximum(np.where(amax > 0, np.frexp(amax)[1] - 1 + 127, 0) - down, 1)
    scale = np.exp2(byte - 127.0)
    codes = (blocks / scale).astype(np.float32).astype(dtype).astype(np.float64)
    return np.moveaxis((codes * scale).reshape(v.shape), -1, axis)


WIDE = False


def mx_kscale(k):
    if not WIDE:
        return np.ones(k)
    levels = np.array([10, -10, 5, -5, 0])
    if k % 512:
        return np.exp2(np.random.permutation(np.resize(levels, k // 32))).repeat(32)
    a = np.empty((k // 512, 16))
    for p in range(k // 512):
        a[p, :8] = np.random.permutation(np.resize(levels, 8))
        for g in range(8):
            far = levels[np.abs(levels - a[p, g]) >= 10]
            a[p, g + 8] = far[np.random.randint(len(far))]
    return np.exp2(a.ravel()).repeat(32)


BF16 = ml_dtypes.bfloat16


def bf(x):
    return np.asarray(x, np.float32).astype(BF16)


def f64(x):
    return np.asarray(x).astype(np.float64)


B, P, K, D, L, C0, C1, C2, C3 = 2048, 64, 128, 512, 4, 256, 512, 1024, 2048
C = C3
F = 2 * C
EPS = 1e-5


def layernorm(x, g, b):
    m = x.mean(axis=-1, keepdims=True)
    v = x.var(axis=-1, keepdims=True)
    return (x - m) / np.sqrt(v + EPS) * g + b


def l2norm(x):
    n = np.sqrt((x * x).sum(axis=-1, keepdims=True))
    return x / np.maximum(n, 1e-12)


def setup_inputs():
    s = mx_kscale(F)
    return {"pooled": bf(0.5 + 2.0 * np.random.standard_normal((B, C))),
            "proto": bf(np.random.standard_normal((1, C)) + np.random.standard_normal((P, C))),
            "ln_g": bf((1.0 + 0.1 * np.random.standard_normal(F)) * s),
            "ln_b": bf(0.1 * np.random.standard_normal(F) * s),
            "W": bf(np.random.standard_normal((F, D)) / np.sqrt(F) / s[:, None]),
            "b": bf(0.1 * np.random.standard_normal(D))}


def reference(pooled, proto, ln_g, ln_b, W, b):
    pl = f64(pooled)
    proto_ctx = np.broadcast_to(f64(proto).mean(axis=0, keepdims=True), pl.shape)
    fused = np.concatenate([pl, proto_ctx], axis=1)
    z = layernorm(fused, f64(ln_g), f64(ln_b))
    h = np.maximum((mxq(z, 1, "e4m3") @ mxq(f64(W), 0, "e4m3")) + f64(b), 0.0)
    return l2norm(h)

@@ -1,0 +1,352 @@
+from contextlib import ExitStack
+
+import concourse.mybir as mybir
+from concourse.masks import make_identity
+
+F32 = mybir.dt.float32
+BF16 = mybir.dt.bfloat16
+U32 = mybir.dt.uint32
+U8 = mybir.dt.uint8
+FP8X4 = mybir.dt.float8_e4m3fn_x4
+ACT = mybir.ActivationFunctionType
+ALU = mybir.AluOpType
+
+P = 128
+PACK = 4
+K_PASS = P * PACK
+ROWS = 2048
+CHANNELS = 2048
+PROTOS = 64
+FUSED = 2 * CHANNELS
+D_OUT = 512
+EPS = 1e-5
+TINY_NORM = 1e-12
+
+PASSES = FUSED // K_PASS
+GROUP_TILES = 4
+GROUP_ROWS = GROUP_TILES * P
+GROUPS = ROWS // GROUP_ROWS
+STAT_WIDTH = 512
+STATS_PER_HALF = CHANNELS // STAT_WIDTH
+SLAB = 1024
+SLAB_PASSES = SLAB // K_PASS
+SLABS = FUSED // SLAB
+TOTAL_PASSES = GROUPS * PASSES
+NORMALISE_AHEAD = 4
+REGROUP_LAG = 1
+QUANTISE_LAG = 2
+MULTIPLY_LAG = 3
+NORMS_LAG = 4
+STORE_LAG = 5
+W_AHEAD = 4
+
+FLOPS = 2 * ROWS * FUSED * D_OUT
+
+
+def regroup(copy, planes, grouped):
+    copy(
+        out=grouped[:].rearrange("p (c i) t -> p c t i", i=4),
+        in_=planes[:].rearrange("p t (c i) -> p c t i", i=4),
+    )
+
+
+def quantise(nc, grouped, codes, scales):
+    nc.vector.quantize_mx(
+        out=codes.bitcast(FP8X4), scales=scales, in_=grouped[:].rearrange("p w t -> p (w t)")
+    )
+
+
+def tile_textguidedcamfusion_pa_kernel(tc, pooled, proto, ln_g, ln_b, W, b, out):
+    nc = tc.nc
+    with ExitStack() as stack:
+        const = stack.enter_context(tc.tile_pool(name="const", bufs=1))
+        x_pool = stack.enter_context(tc.tile_pool(name="x", bufs=2 * GROUP_TILES))
+        w_stage = stack.enter_context(tc.tile_pool(name="w_stage", bufs=2))
+        y_pool = stack.enter_context(tc.tile_pool(name="y", bufs=3))
+        z_stage = stack.enter_context(tc.tile_pool(name="z_stage", bufs=3))
+        z_words = stack.enter_context(tc.tile_pool(name="z_words", bufs=3))
+        small = stack.enter_context(tc.tile_pool(name="small", bufs=2))
+        tail = stack.enter_context(tc.tile_pool(name="tail", bufs=GROUP_TILES))
+        flip_psum = stack.enter_context(tc.psum_pool(name="flip_psum", bufs=4))
+        acc_psum = stack.enter_context(tc.psum_pool(name="acc_psum", bufs=GROUP_TILES))
+
+        x_tiles = {}
+
+        def load_group(s):
+            for rt in range(s * GROUP_TILES, (s + 1) * GROUP_TILES):
+                x_tile = x_pool.tile([P, CHANNELS], BF16, name="x_tile")
+                nc.sync.dma_start(out=x_tile[:], in_=pooled[rt * P : (rt + 1) * P, :])
+                x_tiles[rt] = x_tile
+
+        load_group(0)
+
+        gain_shift_rows = const.tile([P, K_PASS], BF16)
+        nc.vector.memset(gain_shift_rows[:], 0.0)
+        nc.scalar.dma_start(out=gain_shift_rows[0:PASSES, :], in_=ln_g.rearrange("(g k) -> g k", k=K_PASS))
+        nc.scalar.dma_start(
+            out=gain_shift_rows[PASSES : 2 * PASSES, :], in_=ln_b.rearrange("(g k) -> g k", k=K_PASS)
+        )
+        proto_rows = const.tile([P, CHANNELS], BF16)
+        nc.vector.memset(proto_rows[PROTOS:P, :], 0.0)
+        nc.scalar.dma_start(out=proto_rows[0:PROTOS, :], in_=proto)
+        bias_rows = const.tile([P, D_OUT], BF16)
+        nc.scalar.dma_start(out=bias_rows[:], in_=b.partition_broadcast(P))
+
+        w_view = W.rearrange("(g p t) n -> g p t n", t=PACK, p=P)
+        w_planes = {}
+
+        def load_w(g):
+            w_plane = w_stage.tile([P, PACK, D_OUT], BF16, name="w_plane", bufs=W_AHEAD)
+            nc.sync.dma_start(out=w_plane[:], in_=w_view[g])
+            w_planes[g] = w_plane
+
+        for g in range(W_AHEAD):
+            load_w(g)
+        load_group(1)
+
+        identity = const.tile([P, P], F32)
+        make_identity(nc, identity[:])
+        ones = const.tile([P, P], BF16)
+        nc.vector.memset(ones[:], 1.0)
+        eps = const.tile([P, 1], F32)
+        nc.vector.memset(eps[:], EPS)
+
+        gain_shift_f32 = const.tile([P, PACK, P], F32)
+        nc.vector.tensor_copy(
+            out=gain_shift_f32[:], in_=gain_shift_rows[:].rearrange("r (p t) -> r t p", t=PACK)
+        )
+        gain_shift_bank = flip_psum.tile([P, GROUP_ROWS], F32, name="bank")
+        for t in range(PACK):
+            nc.tensor.transpose(
+                gain_shift_bank[:, t * P : (t + 1) * P], gain_shift_f32[:, t, :], identity[:]
+            )
+        gain_shift = const.tile([P, PACK, 2 * PASSES], F32)
+        nc.vector.tensor_copy(
+            out=gain_shift[:],
+            in_=gain_shift_bank[:].rearrange("p (t r) -> p t r", t=PACK)[:, :, 0 : 2 * PASSES],
+        )
+
+        context = const.tile([P, CHANNELS], F32)
+        context_stats = const.tile([P, STATS_PER_HALF, 6], F32)
+        for j in range(STATS_PER_HALF):
+            cols = slice(j * STAT_WIDTH, (j + 1) * STAT_WIDTH)
+            sum_bank = flip_psum.tile([P, GROUP_ROWS], F32, name="bank")
+            nc.tensor.matmul(sum_bank[:], lhsT=ones[:], rhs=proto_rows[:, cols], start=True, stop=True)
+            nc.scalar.activation(
+                out=context[:, cols].rearrange("p (t w) -> p t w", t=PACK),
+                in_=sum_bank[:].rearrange("p (w t) -> p t w", t=PACK),
+                func=ACT.Copy,
+                scale=1.0 / PROTOS,
+            )
+            nc.vector.bn_stats(out=context_stats[:, j, :], in_=context[:, cols])
+
+        stats = const.tile([P, GROUPS * GROUP_TILES, 2 * STATS_PER_HALF, 6], F32)
+        nc.vector.tensor_copy(
+            out=stats[:, :, STATS_PER_HALF:, :],
+            in_=context_stats[:].unsqueeze(1).to_broadcast([P, GROUPS * GROUP_TILES, STATS_PER_HALF, 6]),
+        )
+
+        w_codes = const.tile([P, PASSES, D_OUT], U32, align_bytes=64)
+        w_scales = const.tile([P, PASSES, D_OUT], U8, align_bytes=64)
+
+        def quantise_w(g):
+            w_grouped = w_stage.tile([P, D_OUT, PACK], BF16, align_bytes=64, name="w_grouped")
+            regroup(nc.scalar.copy, w_planes[g], w_grouped)
+            quantise(nc, w_grouped, w_codes[:, g, :], w_scales[:, g, :])
+            if g + W_AHEAD < PASSES:
+                load_w(g + W_AHEAD)
+
+        row_scale = {}
+
+        mean_vars = {}
+
+        def tile_statistics(s, r):
+            if r == 0:
+                mean_vars[s] = small.tile([P, GROUP_TILES, 2], F32, name="mean_var")
+            rt = s * GROUP_TILES + r
+            for j in range(STATS_PER_HALF):
+                cols = slice(j * STAT_WIDTH, (j + 1) * STAT_WIDTH)
+                nc.vector.bn_stats(out=stats[:, rt, j, :], in_=x_tiles[rt][:, cols])
+            nc.vector.bn_aggr(
+                out=mean_vars[s][:, r, :], in_=stats[:, rt, :, :].rearrange("p j v -> p (j v)")
+            )
+
+        def group_scales(s):
+            mean_var = mean_vars[s]
+            rstd = small.tile([P, GROUP_TILES], F32, name="rstd")
+            nc.scalar.activation(out=rstd[:], in_=mean_var[:, :, 1], func=ACT.Sqrt, bias=eps[:])
+            nc.vector.reciprocal(out=rstd[:], in_=rstd[:])
+            shift = small.tile([P, GROUP_TILES], F32, name="shift")
+            nc.vector.scalar_tensor_tensor(
+                out=shift[:], in0=mean_var[:, :, 0], scalar=-1.0, in1=rstd[:], op0=ALU.mult, op1=ALU.mult
+            )
+            row_scale[s] = (rstd, shift)
+
+        y_slabs = {}
+
+        def normalise(s, slab, row_tiles):
+            rstd, shift = row_scale[s]
+            first = slab * SLAB
+            if row_tiles[0] == 0:
+                y_slabs[(s, slab)] = y_pool.tile([P, GROUP_TILES, SLAB], F32, name="y")
+            y = y_slabs[(s, slab)]
+            for r in row_tiles:
+                if first < CHANNELS:
+                    nc.vector.tensor_scalar(
+                        out=y[:, r, :].rearrange("p (h t w) -> p h t w", t=PACK, w=P),
+                        in0=x_tiles[s * GROUP_TILES + r][:, first : first + SLAB].rearrange(
+                            "p (h w t) -> p h t w", t=PACK, w=P
+                        ),
+                        scalar1=rstd[:, r : r + 1],
+                        scalar2=shift[:, r : r + 1],
+                        op0=ALU.mult,
+                        op1=ALU.add,
+                    )
+                else:
+                    nc.scalar.activation(
+                        out=y[:, r, :],
+                        in_=context[:, first - CHANNELS : first - CHANNELS + SLAB],
+                        func=ACT.Identity,
+                        scale=rstd[:, r : r + 1],
+                        bias=shift[:, r : r + 1],
+                    )
+
+        def flip(s, g):
+            y = y_slabs[(s, g // SLAB_PASSES)]
+            z_planes = z_stage.tile([P, PACK, GROUP_ROWS], BF16, name="z_planes")
+            for t in range(PACK):
+                c = g * PACK + t
+                first = (c * P) % SLAB
+                bank = flip_psum.tile([P, GROUP_ROWS], F32, name="bank")
+                for r in range(GROUP_TILES):
+                    nc.tensor.transpose(
+                        bank[:, r * P : (r + 1) * P], y[:, r, first : first + P], identity[:]
+                    )
+                nc.scalar.activation(
+                    out=z_planes[:, t, :],
+                    in_=bank[:],
+                    func=ACT.Identity,
+                    scale=gain_shift[:, t, g : g + 1],
+                    bias=gain_shift[:, t, PASSES + g : PASSES + g + 1],
+                )
+            return z_planes
+
+        def regroup_z(z_planes):
+            z_grouped = z_stage.tile([P, GROUP_ROWS, PACK], BF16, align_bytes=64, name="z_grouped")
+            regroup(nc.vector.tensor_copy, z_planes, z_grouped)
+            return z_grouped
+
+        def quantise_z(z_grouped):
+            z_codes = z_words.tile([P, GROUP_ROWS], U32, align_bytes=64, name="z_codes")
+            z_scales = z_words.tile([P, GROUP_ROWS], U8, align_bytes=64, name="z_scales")
+            quantise(nc, z_grouped, z_codes[:], z_scales[:])
+            return z_codes, z_scales
+
+        accs_of = {}
+
+        def multiply(s, g, z_codes, z_scales):
+            if g == 0:
+                accs_of[s] = []
+                for r in range(GROUP_TILES):
+                    acc = acc_psum.tile([P, D_OUT], F32, name="acc")
+                    accs_of[s].append(acc)
+            accs = accs_of[s]
+            for r in range(GROUP_TILES):
+                rows = slice(r * P, (r + 1) * P)
+                nc.tensor.matmul_mx(
+                    out=accs[r][:],
+                    lhsT=z_codes[:, rows].bitcast(FP8X4),
+                    lhsT_scale=z_scales[:, rows],
+                    rhs=w_codes[:, g, :].bitcast(FP8X4),
+                    rhs_scale=w_scales[:, g, :],
+                    start=(g == 0),
+                    stop=(g == PASSES - 1),
+                )
+
+        hs_of = {}
+        inverse_norms = {}
+
+        def add_bias(s):
+            hs_of[s] = []
+            for r in range(GROUP_TILES):
+                h = tail.tile([P, D_OUT], F32, name="h", bufs=2 * GROUP_TILES)
+                nc.vector.tensor_tensor(out=h[:], in0=accs_of[s][r][:], in1=bias_rows[:], op=ALU.add)
+                hs_of[s].append(h)
+
+        def norms(s):
+            square_sum = small.tile([P, GROUP_TILES], F32, name="square_sum")
+            for r in range(GROUP_TILES):
+                squares = tail.tile([P, D_OUT], F32, name="squares", bufs=2)
+                nc.vector.scalar_tensor_tensor(
+                    out=squares[:],
+                    in0=hs_of[s][r][:],
+                    scalar=0.0,
+                    in1=hs_of[s][r][:],
+                    op0=ALU.max,
+                    op1=ALU.mult,
+                    accum_out=square_sum[:, r : r + 1],
+                )
+            inverse_norm = small.tile([P, GROUP_TILES], F32, name="inverse_norm")
+            nc.scalar.activation(out=inverse_norm[:], in_=square_sum[:], func=ACT.Sqrt)
+            nc.vector.tensor_scalar_max(out=inverse_norm[:], in0=inverse_norm[:], scalar1=TINY_NORM)
+            nc.vector.reciprocal(out=inverse_norm[:], in_=inverse_norm[:])
+            inverse_norms[s] = inverse_norm
+
+        def scale_and_store(s):
+            for r in range(GROUP_TILES):
+                rt = s * GROUP_TILES + r
+                h = hs_of[s][r]
+                nc.vector.tensor_scalar(
+                    out=h[:],
+                    in0=h[:],
+                    scalar1=0.0,
+                    scalar2=inverse_norms[s][:, r : r + 1],
+                    op0=ALU.max,
+                    op1=ALU.mult,
+                )
+                nc.sync.dma_start(out=out[rt * P : (rt + 1) * P, :], in_=h[:])
+
+        all_tiles = list(range(GROUP_TILES))
+        half_tiles = GROUP_TILES // SLAB_PASSES
+        for r in all_tiles:
+            tile_statistics(0, r)
+        group_scales(0)
+        for slab in range(NORMALISE_AHEAD // SLAB_PASSES):
+            normalise(0, slab, all_tiles)
+
+        z_planes_of = {}
+        z_grouped_of = {}
+        z_words_of = {}
+        for step in range(TOTAL_PASSES + STORE_LAG + 1):
+            multiplied = step - MULTIPLY_LAG
+            if 0 <= multiplied < TOTAL_PASSES:
+                s, g = divmod(multiplied, PASSES)
+                multiply(s, g, *z_words_of[multiplied])
+                if g == PASSES - 1:
+                    add_bias(s)
+            if step < TOTAL_PASSES:
+                s, g = divmod(step, PASSES)
+                if g == 0 and s + 2 < GROUPS:
+                    load_group(s + 2)
+                z_planes_of[step] = flip(s, g)
+                if s == 0:
+                    quantise_w(g)
+            if 0 <= step - REGROUP_LAG < TOTAL_PASSES:
+                z_grouped_of[step - REGROUP_LAG] = regroup_z(z_planes_of[step - REGROUP_LAG])
+            if 0 <= step - QUANTISE_LAG < TOTAL_PASSES:
+                z_words_of[step - QUANTISE_LAG] = quantise_z(z_grouped_of[step - QUANTISE_LAG])
+            s, g = divmod(step - NORMS_LAG, PASSES)
+            if 0 <= s < GROUPS and g == PASSES - 1:
+                norms(s)
+            s, g = divmod(step - STORE_LAG, PASSES)
+            if 0 <= s < GROUPS and g == PASSES - 1:
+                scale_and_store(s)
+            if step + NORMALISE_AHEAD < TOTAL_PASSES:
+                s, g = divmod(step + NORMALISE_AHEAD, PASSES)
+                first_tile = (g % SLAB_PASSES) * half_tiles
+                normalise(s, g // SLAB_PASSES, all_tiles[first_tile : first_tile + half_tiles])
+            s, g = divmod(step + PASSES, PASSES)
+            if s < GROUPS and g < GROUP_TILES:
+                tile_statistics(s, g)
+            if s < GROUPS and g == GROUP_TILES - 1:
+                group_scales(s)

@@ -10,6 +10,7 @@ U8 = mybir.dt.uint8
 FP8X4 = mybir.dt.float8_e4m3fn_x4
 ACT = mybir.ActivationFunctionType
 ALU = mybir.AluOpType
+AXIS = mybir.AxisListType
 
 P = 128
 PACK = 4
@@ -23,22 +24,25 @@ EPS = 1e-5
 TINY_NORM = 1e-12
 
 PASSES = FUSED // K_PASS
+X_PASSES = CHANNELS // K_PASS
+OUTER_PASSES = 3
 GROUP_TILES = 4
 GROUP_ROWS = GROUP_TILES * P
 GROUPS = ROWS // GROUP_ROWS
+ROW_TILES = ROWS // P
 STAT_WIDTH = 512
-STATS_PER_HALF = CHANNELS // STAT_WIDTH
+STATS_PER_TILE = CHANNELS // STAT_WIDTH
 SLAB = 1024
 SLAB_PASSES = SLAB // K_PASS
-SLABS = FUSED // SLAB
+PIECES = 3
+SLOTS = 4
+ONE_SLOT = PIECES * SLOTS
 TOTAL_PASSES = GROUPS * PASSES
-NORMALISE_AHEAD = 4
+ORDER = [g for pair in zip(range(X_PASSES), range(X_PASSES, PASSES)) for g in pair]
 REGROUP_LAG = 1
 QUANTISE_LAG = 2
 MULTIPLY_LAG = 3
-NORMS_LAG = 4
-STORE_LAG = 5
-W_AHEAD = 4
+W_AHEAD = 5
 
 FLOPS = 2 * ROWS * FUSED * D_OUT
 
@@ -60,9 +64,9 @@ def tile_textguidedcamfusion_pa_kernel(tc, pooled, proto, ln_g, ln_b, W, b, out)
     nc = tc.nc
     with ExitStack() as stack:
         const = stack.enter_context(tc.tile_pool(name="const", bufs=1))
-        x_pool = stack.enter_context(tc.tile_pool(name="x", bufs=2 * GROUP_TILES))
-        w_stage = stack.enter_context(tc.tile_pool(name="w_stage", bufs=2))
-        y_pool = stack.enter_context(tc.tile_pool(name="y", bufs=3))
+        x_pool = stack.enter_context(tc.tile_pool(name="x", bufs=ROW_TILES))
+        w_stage = stack.enter_context(tc.tile_pool(name="w_stage", bufs=3))
+        y_pool = stack.enter_context(tc.tile_pool(name="y", bufs=2))
         z_stage = stack.enter_context(tc.tile_pool(name="z_stage", bufs=3))
         z_words = stack.enter_context(tc.tile_pool(name="z_words", bufs=3))
         small = stack.enter_context(tc.tile_pool(name="small", bufs=2))
@@ -82,34 +86,65 @@ def tile_textguidedcamfusion_pa_kernel(tc, pooled, proto, ln_g, ln_b, W, b, out)
 
         gain_shift_rows = const.tile([P, K_PASS], BF16)
         nc.vector.memset(gain_shift_rows[:], 0.0)
+        proto_rows = const.tile([P, CHANNELS], BF16)
+        nc.vector.memset(proto_rows[PROTOS:P, :], 0.0)
+        nc.scalar.dma_start(out=proto_rows[0:PROTOS, :], in_=proto)
         nc.scalar.dma_start(out=gain_shift_rows[0:PASSES, :], in_=ln_g.rearrange("(g k) -> g k", k=K_PASS))
         nc.scalar.dma_start(
             out=gain_shift_rows[PASSES : 2 * PASSES, :], in_=ln_b.rearrange("(g k) -> g k", k=K_PASS)
         )
-        proto_rows = const.tile([P, CHANNELS], BF16)
-        nc.vector.memset(proto_rows[PROTOS:P, :], 0.0)
-        nc.scalar.dma_start(out=proto_rows[0:PROTOS, :], in_=proto)
-        bias_rows = const.tile([P, D_OUT], BF16)
-        nc.scalar.dma_start(out=bias_rows[:], in_=b.partition_broadcast(P))
 
         w_view = W.rearrange("(g p t) n -> g p t n", t=PACK, p=P)
         w_planes = {}
 
-        def load_w(g):
+        def load_w(n):
             w_plane = w_stage.tile([P, PACK, D_OUT], BF16, name="w_plane", bufs=W_AHEAD)
-            nc.sync.dma_start(out=w_plane[:], in_=w_view[g])
-            w_planes[g] = w_plane
+            nc.sync.dma_start(out=w_plane[:], in_=w_view[ORDER[n]])
+            w_planes[n] = w_plane
 
-        for g in range(W_AHEAD):
-            load_w(g)
-        load_group(1)
+        for n in range(W_AHEAD):
+            load_w(n)
+        for s in range(1, GROUPS):
+            load_group(s)
+        bias_rows = const.tile([P, D_OUT], BF16)
+        nc.scalar.dma_start(out=bias_rows[:], in_=b.partition_broadcast(P))
 
         identity = const.tile([P, P], F32)
         make_identity(nc, identity[:])
+        identity_bf = const.tile([P, P], BF16)
+        make_identity(nc, identity_bf[:])
         ones = const.tile([P, P], BF16)
-        nc.vector.memset(ones[:], 1.0)
+        nc.gpsimd.memset(ones[:], 1.0)
+        ones_f32 = const.tile([P, P], F32)
+        nc.gpsimd.memset(ones_f32[:], 1.0)
         eps = const.tile([P, 1], F32)
-        nc.vector.memset(eps[:], EPS)
+        nc.gpsimd.memset(eps[:], EPS)
+        k_terms_in = const.tile([P, PACK, X_PASSES, P], BF16)
+        nc.gpsimd.memset(k_terms_in[:], 0.0)
+        row_terms_in = []
+        for i in range(2):
+            row_terms = const.tile([P, GROUP_TILES, P], BF16, name="row_terms_" + str(i))
+            nc.gpsimd.memset(row_terms[:], 0.0)
+            nc.vector.memset(row_terms[:, :, ONE_SLOT : ONE_SLOT + 1], 1.0)
+            row_terms_in.append(row_terms)
+
+        sum_bank = flip_psum.tile([P, GROUP_ROWS], F32, name="bank")
+        for t in range(PACK):
+            for q in range(X_PASSES):
+                n = t * X_PASSES + q
+                nc.tensor.matmul(
+                    sum_bank[:, n : n + 1],
+                    lhsT=proto_rows[:, q * K_PASS + t : (q + 1) * K_PASS : PACK],
+                    rhs=ones[:, 0:1],
+                    start=True,
+                    stop=True,
+                )
+        context_k = const.tile([P, PACK, X_PASSES], F32)
+        nc.vector.tensor_scalar_mul(
+            out=context_k[:].rearrange("p t q -> p (t q)"),
+            in0=sum_bank[:, 0 : PACK * X_PASSES],
+            scalar1=1.0 / PROTOS,
+        )
 
         gain_shift_f32 = const.tile([P, PACK, P], F32)
         nc.vector.tensor_copy(
@@ -126,101 +161,186 @@ def tile_textguidedcamfusion_pa_kernel(tc, pooled, proto, ln_g, ln_b, W, b, out)
             in_=gain_shift_bank[:].rearrange("p (t r) -> p t r", t=PACK)[:, :, 0 : 2 * PASSES],
         )
 
-        context = const.tile([P, CHANNELS], F32)
-        context_stats = const.tile([P, STATS_PER_HALF, 6], F32)
-        for j in range(STATS_PER_HALF):
-            cols = slice(j * STAT_WIDTH, (j + 1) * STAT_WIDTH)
-            sum_bank = flip_psum.tile([P, GROUP_ROWS], F32, name="bank")
-            nc.tensor.matmul(sum_bank[:], lhsT=ones[:], rhs=proto_rows[:, cols], start=True, stop=True)
-            nc.scalar.activation(
-                out=context[:, cols].rearrange("p (t w) -> p t w", t=PACK),
-                in_=sum_bank[:].rearrange("p (w t) -> p t w", t=PACK),
-                func=ACT.Copy,
-                scale=1.0 / PROTOS,
-            )
-            nc.vector.bn_stats(out=context_stats[:, j, :], in_=context[:, cols])
+        context_stats = const.tile([P, 3], F32)
+        nc.vector.memset(context_stats[:, 0:1], float(CHANNELS))
 
-        stats = const.tile([P, GROUPS * GROUP_TILES, 2 * STATS_PER_HALF, 6], F32)
-        nc.vector.tensor_copy(
-            out=stats[:, :, STATS_PER_HALF:, :],
-            in_=context_stats[:].unsqueeze(1).to_broadcast([P, GROUPS * GROUP_TILES, STATS_PER_HALF, 6]),
+        def sum_everywhere(values, name):
+            bank = flip_psum.tile([P, GROUP_ROWS], F32, name="bank")
+            nc.tensor.matmul(
+                bank[:, 0 : PACK * X_PASSES],
+                lhsT=ones_f32[:],
+                rhs=values[:].rearrange("p t q -> p (t q)"),
+                start=True,
+                stop=True,
+            )
+            total = const.tile([P, 1], F32, name=name)
+            nc.vector.tensor_reduce(out=total[:], in_=bank[:, 0 : PACK * X_PASSES], op=ALU.add, axis=AXIS.X)
+            return total
+
+        context_sum = sum_everywhere(context_k, "context_sum")
+        nc.vector.tensor_scalar_mul(out=context_stats[:, 1:2], in0=context_sum[:], scalar1=1.0 / CHANNELS)
+        centred = const.tile([P, PACK, X_PASSES], F32)
+        nc.vector.tensor_scalar(
+            out=centred[:], in0=context_k[:], scalar1=context_stats[:, 1:2], scalar2=None, op0=ALU.subtract
         )
+        nc.vector.tensor_tensor(out=centred[:], in0=centred[:], in1=centred[:], op=ALU.mult)
+        squared_sum = sum_everywhere(centred, "squared_sum")
+        nc.vector.tensor_copy(out=context_stats[:, 2:3], in_=squared_sum[:])
+
+        own = 6 * STATS_PER_TILE
+        stats = const.tile([P, ROW_TILES, own + 3], F32)
+        nc.vector.tensor_copy(
+            out=stats[:, :, own : own + 3],
+            in_=context_stats[:].unsqueeze(1).to_broadcast([P, ROW_TILES, 3]),
+        )
+
+        context_row = const.tile([P, K_PASS], F32)
+        row_bank = flip_psum.tile([P, GROUP_ROWS], F32, name="bank")
+        nc.tensor.matmul(
+            row_bank[:], lhsT=ones[:], rhs=proto_rows[:, OUTER_PASSES * K_PASS :], start=True, stop=True
+        )
+        nc.scalar.activation(
+            out=context_row[:].rearrange("p (t w) -> p t w", t=PACK),
+            in_=row_bank[:].rearrange("p (w t) -> p t w", t=PACK),
+            func=ACT.Copy,
+            scale=1.0 / PROTOS,
+        )
+
+        k_pieces = const.tile([P, PACK, X_PASSES, SLOTS], BF16)
+        rest = const.tile([P, PACK, X_PASSES], F32)
+        nc.vector.tensor_tensor(
+            out=rest[:], in0=context_k[:], in1=gain_shift[:, :, X_PASSES:PASSES], op=ALU.mult
+        )
+        for u in range(PIECES):
+            nc.vector.tensor_copy(out=k_pieces[:, :, :, u], in_=rest[:])
+            if u + 1 < PIECES:
+                nc.vector.tensor_tensor(out=rest[:], in0=rest[:], in1=k_pieces[:, :, :, u], op=ALU.subtract)
+        nc.vector.tensor_copy(out=k_pieces[:, :, :, PIECES], in_=gain_shift[:, :, X_PASSES:PASSES])
+        for j in range(PIECES):
+            nc.vector.tensor_copy(out=k_terms_in[:, :, :, j * SLOTS : (j + 1) * SLOTS], in_=k_pieces[:])
+        nc.vector.tensor_copy(
+            out=k_terms_in[:, :, :, ONE_SLOT], in_=gain_shift[:, :, PASSES + X_PASSES : 2 * PASSES]
+        )
+        k_terms = const.tile([P, OUTER_PASSES, PACK, P], BF16)
+        for q in range(OUTER_PASSES):
+            bank = flip_psum.tile([P, PACK, P], BF16, name="bank")
+            for t in range(PACK):
+                nc.tensor.transpose(bank[:, t, :], k_terms_in[:, t, q, :], identity_bf[:])
+            nc.scalar.copy(out=k_terms[:, q, :, :], in_=bank[:])
 
         w_codes = const.tile([P, PASSES, D_OUT], U32, align_bytes=64)
         w_scales = const.tile([P, PASSES, D_OUT], U8, align_bytes=64)
 
-        def quantise_w(g):
+        def quantise_w(n):
             w_grouped = w_stage.tile([P, D_OUT, PACK], BF16, align_bytes=64, name="w_grouped")
-            regroup(nc.scalar.copy, w_planes[g], w_grouped)
-            quantise(nc, w_grouped, w_codes[:, g, :], w_scales[:, g, :])
-            if g + W_AHEAD < PASSES:
-                load_w(g + W_AHEAD)
+            regroup(nc.scalar.copy, w_planes[n], w_grouped)
+            quantise(nc, w_grouped, w_codes[:, ORDER[n], :], w_scales[:, ORDER[n], :])
+            if n + W_AHEAD < PASSES:
+                load_w(n + W_AHEAD)
+
+        def tile_statistics(rt, j):
+            cols = slice(j * STAT_WIDTH, (j + 1) * STAT_WIDTH)
+            nc.vector.bn_stats(out=stats[:, rt, 6 * j : 6 * (j + 1)], in_=x_tiles[rt][:, cols])
 
         row_scale = {}
 
-        mean_vars = {}
-
-        def tile_statistics(s, r):
-            if r == 0:
-                mean_vars[s] = small.tile([P, GROUP_TILES, 2], F32, name="mean_var")
-            rt = s * GROUP_TILES + r
-            for j in range(STATS_PER_HALF):
-                cols = slice(j * STAT_WIDTH, (j + 1) * STAT_WIDTH)
-                nc.vector.bn_stats(out=stats[:, rt, j, :], in_=x_tiles[rt][:, cols])
-            nc.vector.bn_aggr(
-                out=mean_vars[s][:, r, :], in_=stats[:, rt, :, :].rearrange("p j v -> p (j v)")
-            )
-
         def group_scales(s):
-            mean_var = mean_vars[s]
-            rstd = small.tile([P, GROUP_TILES], F32, name="rstd")
-            nc.scalar.activation(out=rstd[:], in_=mean_var[:, :, 1], func=ACT.Sqrt, bias=eps[:])
-            nc.vector.reciprocal(out=rstd[:], in_=rstd[:])
-            shift = small.tile([P, GROUP_TILES], F32, name="shift")
-            nc.vector.scalar_tensor_tensor(
-                out=shift[:], in0=mean_var[:, :, 0], scalar=-1.0, in1=rstd[:], op0=ALU.mult, op1=ALU.mult
+            mean_var = small.tile([P, GROUP_TILES, 2], F32, name="mean_var")
+            for r in range(GROUP_TILES):
+                nc.vector.bn_aggr(out=mean_var[:, r, :], in_=stats[:, s * GROUP_TILES + r, :])
+            std = small.tile([P, GROUP_TILES], F32, name="std")
+            nc.scalar.activation(out=std[:], in_=mean_var[:, :, 1], func=ACT.Sqrt, bias=eps[:])
+            scale = small.tile([P, GROUP_TILES, SLOTS], F32, name="scale")
+            nc.vector.reciprocal(
+                out=scale[:, :, 0:PIECES],
+                in_=std[:].unsqueeze(2).to_broadcast([P, GROUP_TILES, PIECES]),
             )
-            row_scale[s] = (rstd, shift)
+            nc.vector.scalar_tensor_tensor(
+                out=scale[:, :, PIECES],
+                in0=mean_var[:, :, 0],
+                scalar=-1.0,
+                in1=scale[:, :, 0],
+                op0=ALU.mult,
+                op1=ALU.mult,
+            )
+            row_scale[s] = scale
+
+        row_terms_of = {}
+
+        def split_rows(s):
+            terms = row_terms_in[s % 2]
+            left = row_scale[s]
+            for j in range(PIECES):
+                piece = terms[:, :, j * SLOTS : (j + 1) * SLOTS]
+                nc.vector.tensor_copy(out=piece, in_=left[:])
+                if j + 1 < PIECES:
+                    rest_of_rows = small.tile([P, GROUP_TILES, SLOTS], F32, name="rest_of_rows")
+                    nc.vector.tensor_tensor(out=rest_of_rows[:], in0=left[:], in1=piece, op=ALU.subtract)
+                    left = rest_of_rows
+
+        def flip_rows(s):
+            bank = flip_psum.tile([P, GROUP_TILES, P], BF16, name="bank")
+            for r in range(GROUP_TILES):
+                nc.tensor.transpose(bank[:, r, :], row_terms_in[s % 2][:, r, :], identity_bf[:])
+            row_terms = small.tile([P, GROUP_ROWS], BF16, name="row_terms")
+            nc.scalar.copy(out=row_terms[:], in_=bank[:].rearrange("p r i -> p (r i)"))
+            row_terms_of[s] = row_terms
 
         y_slabs = {}
 
-        def normalise(s, slab, row_tiles):
-            rstd, shift = row_scale[s]
-            first = slab * SLAB
-            if row_tiles[0] == 0:
+        def normalise_pooled(s, slab, r):
+            if r == 0:
                 y_slabs[(s, slab)] = y_pool.tile([P, GROUP_TILES, SLAB], F32, name="y")
-            y = y_slabs[(s, slab)]
-            for r in row_tiles:
-                if first < CHANNELS:
-                    nc.vector.tensor_scalar(
-                        out=y[:, r, :].rearrange("p (h t w) -> p h t w", t=PACK, w=P),
-                        in0=x_tiles[s * GROUP_TILES + r][:, first : first + SLAB].rearrange(
-                            "p (h w t) -> p h t w", t=PACK, w=P
-                        ),
-                        scalar1=rstd[:, r : r + 1],
-                        scalar2=shift[:, r : r + 1],
-                        op0=ALU.mult,
-                        op1=ALU.add,
-                    )
-                else:
-                    nc.scalar.activation(
-                        out=y[:, r, :],
-                        in_=context[:, first - CHANNELS : first - CHANNELS + SLAB],
-                        func=ACT.Identity,
-                        scale=rstd[:, r : r + 1],
-                        bias=shift[:, r : r + 1],
-                    )
+            scale = row_scale[s]
+            source = x_tiles[s * GROUP_TILES + r][:, slab * SLAB : (slab + 1) * SLAB].rearrange(
+                "p (h w t) -> p h t w", t=PACK, w=P
+            )
+            target = y_slabs[(s, slab)][:, r, :].rearrange("p (h t w) -> p h t w", t=PACK, w=P)
+            if r < GROUP_TILES - 1:
+                nc.vector.tensor_scalar(
+                    out=target,
+                    in0=source,
+                    scalar1=scale[:, r, 0:1],
+                    scalar2=scale[:, r, PIECES : PIECES + 1],
+                    op0=ALU.mult,
+                    op1=ALU.add,
+                )
+            else:
+                nc.scalar.activation(
+                    out=target,
+                    in_=source,
+                    func=ACT.Identity,
+                    scale=scale[:, r, 0:1],
+                    bias=scale[:, r, PIECES : PIECES + 1],
+                )
+
+        def normalise_context(s, r):
+            if r == 0:
+                y_slabs[(s, PASSES)] = y_pool.tile([P, GROUP_TILES, K_PASS], F32, name="y_context", bufs=1)
+            scale = row_scale[s]
+            nc.scalar.activation(
+                out=y_slabs[(s, PASSES)][:, r, :],
+                in_=context_row[:],
+                func=ACT.Identity,
+                scale=scale[:, r, 0:1],
+                bias=scale[:, r, PIECES : PIECES + 1],
+            )
 
         def flip(s, g):
-            y = y_slabs[(s, g // SLAB_PASSES)]
+            if g < X_PASSES:
+                y = y_slabs[(s, g // SLAB_PASSES)]
+                first = (g % SLAB_PASSES) * K_PASS
+            else:
+                y = y_slabs[(s, PASSES)]
+                first = 0
             z_planes = z_stage.tile([P, PACK, GROUP_ROWS], BF16, name="z_planes")
             for t in range(PACK):
-                c = g * PACK + t
-                first = (c * P) % SLAB
                 bank = flip_psum.tile([P, GROUP_ROWS], F32, name="bank")
                 for r in range(GROUP_TILES):
                     nc.tensor.transpose(
-                        bank[:, r * P : (r + 1) * P], y[:, r, first : first + P], identity[:]
+                        bank[:, r * P : (r + 1) * P],
+                        y[:, r, first + t * P : first + (t + 1) * P],
+                        identity[:],
                     )
                 nc.scalar.activation(
                     out=z_planes[:, t, :],
@@ -230,6 +350,23 @@ def tile_textguidedcamfusion_pa_kernel(tc, pooled, proto, ln_g, ln_b, W, b, out)
                     bias=gain_shift[:, t, PASSES + g : PASSES + g + 1],
                 )
             return z_planes
+
+        def outer(s, g):
+            z_grouped = z_stage.tile([P, GROUP_ROWS, PACK], BF16, align_bytes=64, name="z_grouped")
+            half_rows = GROUP_ROWS // 2
+            for half in range(2):
+                rows = slice(half * half_rows, (half + 1) * half_rows)
+                bank = flip_psum.tile([P, PACK, half_rows], BF16, name="bank")
+                for t in range(PACK):
+                    nc.tensor.matmul(
+                        bank[:, t, :],
+                        lhsT=k_terms[:, g - X_PASSES, t, :],
+                        rhs=row_terms_of[s][:, rows],
+                        start=True,
+                        stop=True,
+                    )
+                nc.scalar.copy(out=z_grouped[:, rows, :], in_=bank[:].rearrange("p t i -> p i t"))
+            return z_grouped
 
         def regroup_z(z_planes):
             z_grouped = z_stage.tile([P, GROUP_ROWS, PACK], BF16, align_bytes=64, name="z_grouped")
@@ -244,26 +381,26 @@ def tile_textguidedcamfusion_pa_kernel(tc, pooled, proto, ln_g, ln_b, W, b, out)
 
         accs_of = {}
 
-        def multiply(s, g, z_codes, z_scales):
-            if g == 0:
+        def multiply(s, n, z_codes, z_scales):
+            if n == 0:
                 accs_of[s] = []
                 for r in range(GROUP_TILES):
                     acc = acc_psum.tile([P, D_OUT], F32, name="acc")
                     accs_of[s].append(acc)
-            accs = accs_of[s]
             for r in range(GROUP_TILES):
                 rows = slice(r * P, (r + 1) * P)
                 nc.tensor.matmul_mx(
-                    out=accs[r][:],
+                    out=accs_of[s][r][:],
                     lhsT=z_codes[:, rows].bitcast(FP8X4),
                     lhsT_scale=z_scales[:, rows],
-                    rhs=w_codes[:, g, :].bitcast(FP8X4),
-                    rhs_scale=w_scales[:, g, :],
-                    start=(g == 0),
-                    stop=(g == PASSES - 1),
+                    rhs=w_codes[:, ORDER[n], :].bitcast(FP8X4),
+                    rhs_scale=w_scales[:, ORDER[n], :],
+                    start=(n == 0),
+                    stop=(n == PASSES - 1),
                 )
 
         hs_of = {}
+        square_sums = {}
         inverse_norms = {}
 
         def add_bias(s):
@@ -273,80 +410,99 @@ def tile_textguidedcamfusion_pa_kernel(tc, pooled, proto, ln_g, ln_b, W, b, out)
                 nc.vector.tensor_tensor(out=h[:], in0=accs_of[s][r][:], in1=bias_rows[:], op=ALU.add)
                 hs_of[s].append(h)
 
+        def square(s, r):
+            if r == 0:
+                square_sums[s] = small.tile([P, GROUP_TILES], F32, name="square_sum")
+            squares = tail.tile([P, D_OUT], F32, name="squares", bufs=2)
+            nc.vector.scalar_tensor_tensor(
+                out=squares[:],
+                in0=hs_of[s][r][:],
+                scalar=0.0,
+                in1=hs_of[s][r][:],
+                op0=ALU.max,
+                op1=ALU.mult,
+                accum_out=square_sums[s][:, r : r + 1],
+            )
+
         def norms(s):
-            square_sum = small.tile([P, GROUP_TILES], F32, name="square_sum")
-            for r in range(GROUP_TILES):
-                squares = tail.tile([P, D_OUT], F32, name="squares", bufs=2)
-                nc.vector.scalar_tensor_tensor(
-                    out=squares[:],
-                    in0=hs_of[s][r][:],
-                    scalar=0.0,
-                    in1=hs_of[s][r][:],
-                    op0=ALU.max,
-                    op1=ALU.mult,
-                    accum_out=square_sum[:, r : r + 1],
-                )
             inverse_norm = small.tile([P, GROUP_TILES], F32, name="inverse_norm")
-            nc.scalar.activation(out=inverse_norm[:], in_=square_sum[:], func=ACT.Sqrt)
+            nc.scalar.activation(out=inverse_norm[:], in_=square_sums[s][:], func=ACT.Sqrt)
             nc.vector.tensor_scalar_max(out=inverse_norm[:], in0=inverse_norm[:], scalar1=TINY_NORM)
             nc.vector.reciprocal(out=inverse_norm[:], in_=inverse_norm[:])
             inverse_norms[s] = inverse_norm
 
-        def scale_and_store(s):
-            for r in range(GROUP_TILES):
-                rt = s * GROUP_TILES + r
-                h = hs_of[s][r]
-                nc.vector.tensor_scalar(
-                    out=h[:],
-                    in0=h[:],
-                    scalar1=0.0,
-                    scalar2=inverse_norms[s][:, r : r + 1],
-                    op0=ALU.max,
-                    op1=ALU.mult,
-                )
-                nc.sync.dma_start(out=out[rt * P : (rt + 1) * P, :], in_=h[:])
+        def scale_and_store(s, r):
+            rt = s * GROUP_TILES + r
+            h = hs_of[s][r]
+            nc.vector.tensor_scalar(
+                out=h[:],
+                in0=h[:],
+                scalar1=0.0,
+                scalar2=inverse_norms[s][:, r : r + 1],
+                op0=ALU.max,
+                op1=ALU.mult,
+            )
+            nc.sync.dma_start(out=out[rt * P : (rt + 1) * P, :], in_=h[:])
 
-        all_tiles = list(range(GROUP_TILES))
-        half_tiles = GROUP_TILES // SLAB_PASSES
+        all_tiles = range(GROUP_TILES)
+        jobs = {}
+
+        def at(step, call, *arguments):
+            jobs.setdefault(step, []).append((call, arguments))
+
+        for s in range(GROUPS):
+            start = s * PASSES
+            for r in all_tiles:
+                if s > 0:
+                    at(start - 4 + r, normalise_pooled, s, 0, r)
+                at(start + r, normalise_pooled, s, 1, r)
+                at(start + 2 + r, normalise_context, s, r)
+            if s > 0:
+                stat_steps = 4 if s == 1 else 8
+                parts = [(rt, j) for rt in range(s * 4, s * 4 + 4) for j in range(STATS_PER_TILE)]
+                for i, (rt, j) in enumerate(parts):
+                    at(start - 4 - stat_steps + i * stat_steps // len(parts), tile_statistics, rt, j)
+                at(start - 5, group_scales, s)
+                at(start - 4, split_rows, s)
+                at(start - 2, flip_rows, s)
+            done = start + PASSES - 1 + MULTIPLY_LAG
+            at(done, add_bias, s)
+            apart = 1 if s + 1 < GROUPS else 0
+            for r in all_tiles:
+                at(done + 1 + apart * r, square, s, r)
+            at(done + 1 + apart * 4, norms, s)
+            for r in all_tiles:
+                at(done + 1 + apart * (5 + r), scale_and_store, s, r)
+
         for r in all_tiles:
-            tile_statistics(0, r)
+            for j in range(STATS_PER_TILE):
+                tile_statistics(r, j)
         group_scales(0)
-        for slab in range(NORMALISE_AHEAD // SLAB_PASSES):
-            normalise(0, slab, all_tiles)
+        for r in all_tiles:
+            normalise_pooled(0, 0, r)
+        split_rows(0)
+        flip_rows(0)
 
         z_planes_of = {}
         z_grouped_of = {}
         z_words_of = {}
-        for step in range(TOTAL_PASSES + STORE_LAG + 1):
+        for step in range(TOTAL_PASSES + MULTIPLY_LAG + 2):
             multiplied = step - MULTIPLY_LAG
             if 0 <= multiplied < TOTAL_PASSES:
-                s, g = divmod(multiplied, PASSES)
-                multiply(s, g, *z_words_of[multiplied])
-                if g == PASSES - 1:
-                    add_bias(s)
+                s, n = divmod(multiplied, PASSES)
+                multiply(s, n, *z_words_of[multiplied])
             if step < TOTAL_PASSES:
-                s, g = divmod(step, PASSES)
-                if g == 0 and s + 2 < GROUPS:
-                    load_group(s + 2)
-                z_planes_of[step] = flip(s, g)
+                s, n = divmod(step, PASSES)
+                g = ORDER[n]
+                if X_PASSES <= g < X_PASSES + OUTER_PASSES:
+                    z_grouped_of[step] = outer(s, g)
+                else:
+                    z_planes_of[step] = flip(s, g)
                 if s == 0:
-                    quantise_w(g)
-            if 0 <= step - REGROUP_LAG < TOTAL_PASSES:
+                    quantise_w(n)
+            if step - REGROUP_LAG in z_planes_of:
                 z_grouped_of[step - REGROUP_LAG] = regroup_z(z_planes_of[step - REGROUP_LAG])
             if 0 <= step - QUANTISE_LAG < TOTAL_PASSES:
                 z_words_of[step - QUANTISE_LAG] = quantise_z(z_grouped_of[step - QUANTISE_LAG])
-            s, g = divmod(step - NORMS_LAG, PASSES)
-            if 0 <= s < GROUPS and g == PASSES - 1:
-                norms(s)
-            s, g = divmod(step - STORE_LAG, PASSES)
-            if 0 <= s < GROUPS and g == PASSES - 1:
-                scale_and_store(s)
-            if step + NORMALISE_AHEAD < TOTAL_PASSES:
-                s, g = divmod(step + NORMALISE_AHEAD, PASSES)
-                first_tile = (g % SLAB_PASSES) * half_tiles
-                normalise(s, g // SLAB_PASSES, all_tiles[first_tile : first_tile + half_tiles])
-            s, g = divmod(step + PASSES, PASSES)
-            if s < GROUPS and g < GROUP_TILES:
-                tile_statistics(s, g)
-            if s < GROUPS and g == GROUP_TILES - 1:
-                group_scales(s)
+            for call, arguments in jobs.get(step, []):
+                call(*arguments)

@@ -34,15 +34,19 @@ STAT_WIDTH = 512
 STATS_PER_TILE = CHANNELS // STAT_WIDTH
 SLAB = 1024
 SLAB_PASSES = SLAB // K_PASS
+VECTOR_TILES = 2
 PIECES = 3
 SLOTS = 4
 ONE_SLOT = PIECES * SLOTS
 TOTAL_PASSES = GROUPS * PASSES
-ORDER = [g for pair in zip(range(X_PASSES), range(X_PASSES, PASSES)) for g in pair]
+LONG_PASS = PASSES - 1
+CONTEXT_ORDER = (X_PASSES, LONG_PASS, X_PASSES + 1, X_PASSES + 2)
+ORDER = [g for pair in zip(range(X_PASSES), CONTEXT_ORDER) for g in pair]
 REGROUP_LAG = 1
 QUANTISE_LAG = 2
 MULTIPLY_LAG = 3
 W_AHEAD = 5
+W_EARLY = 3
 
 FLOPS = 2 * ROWS * FUSED * D_OUT
 
@@ -64,8 +68,7 @@ def tile_textguidedcamfusion_pa_kernel(tc, pooled, proto, ln_g, ln_b, W, b, out)
     nc = tc.nc
     with ExitStack() as stack:
         const = stack.enter_context(tc.tile_pool(name="const", bufs=1))
-        x_pool = stack.enter_context(tc.tile_pool(name="x", bufs=ROW_TILES))
-        w_stage = stack.enter_context(tc.tile_pool(name="w_stage", bufs=3))
+        stage = stack.enter_context(tc.tile_pool(name="stage", bufs=20))
         y_pool = stack.enter_context(tc.tile_pool(name="y", bufs=2))
         z_stage = stack.enter_context(tc.tile_pool(name="z_stage", bufs=3))
         z_words = stack.enter_context(tc.tile_pool(name="z_words", bufs=3))
@@ -75,58 +78,77 @@ def tile_textguidedcamfusion_pa_kernel(tc, pooled, proto, ln_g, ln_b, W, b, out)
         acc_psum = stack.enter_context(tc.psum_pool(name="acc_psum", bufs=GROUP_TILES))
 
         x_tiles = {}
+        w_planes = {}
+        w_view = W.rearrange("(g p t) n -> g p t n", t=PACK, p=P)
+
+        def load_x(rt):
+            block = stage.tile([P, CHANNELS], BF16, name="block", align_bytes=64)
+            nc.sync.dma_start(out=block[:], in_=pooled[rt * P : (rt + 1) * P, :])
+            x_tiles[rt] = block
+
+        def load_w(n):
+            block = stage.tile([P, PACK, D_OUT], BF16, name="block", align_bytes=64)
+            nc.sync.dma_start(out=block[:], in_=w_view[ORDER[n]])
+            w_planes[n] = block
 
         def load_group(s):
             for rt in range(s * GROUP_TILES, (s + 1) * GROUP_TILES):
-                x_tile = x_pool.tile([P, CHANNELS], BF16, name="x_tile")
-                nc.sync.dma_start(out=x_tile[:], in_=pooled[rt * P : (rt + 1) * P, :])
-                x_tiles[rt] = x_tile
+                load_x(rt)
 
-        load_group(0)
+        for i in range(2):
+            load_x(i)
+            load_w(i)
+        load_x(2)
+        load_x(3)
+        for n in range(2, W_AHEAD):
+            load_w(n)
+        load_group(1)
 
-        gain_shift_rows = const.tile([P, K_PASS], BF16)
-        nc.vector.memset(gain_shift_rows[:], 0.0)
         proto_rows = const.tile([P, CHANNELS], BF16)
         nc.vector.memset(proto_rows[PROTOS:P, :], 0.0)
         nc.scalar.dma_start(out=proto_rows[0:PROTOS, :], in_=proto)
+        gain_shift_rows = const.tile([P, K_PASS], BF16)
+        nc.gpsimd.memset(gain_shift_rows[:], 0.0)
         nc.scalar.dma_start(out=gain_shift_rows[0:PASSES, :], in_=ln_g.rearrange("(g k) -> g k", k=K_PASS))
         nc.scalar.dma_start(
             out=gain_shift_rows[PASSES : 2 * PASSES, :], in_=ln_b.rearrange("(g k) -> g k", k=K_PASS)
         )
-
-        w_view = W.rearrange("(g p t) n -> g p t n", t=PACK, p=P)
-        w_planes = {}
-
-        def load_w(n):
-            w_plane = w_stage.tile([P, PACK, D_OUT], BF16, name="w_plane", bufs=W_AHEAD)
-            nc.sync.dma_start(out=w_plane[:], in_=w_view[ORDER[n]])
-            w_planes[n] = w_plane
-
-        for n in range(W_AHEAD):
-            load_w(n)
-        for s in range(1, GROUPS):
-            load_group(s)
         bias_rows = const.tile([P, D_OUT], BF16)
-        nc.scalar.dma_start(out=bias_rows[:], in_=b.partition_broadcast(P))
 
-        identity = const.tile([P, P], F32)
-        make_identity(nc, identity[:])
-        identity_bf = const.tile([P, P], BF16)
-        make_identity(nc, identity_bf[:])
         ones = const.tile([P, P], BF16)
         nc.gpsimd.memset(ones[:], 1.0)
         ones_f32 = const.tile([P, P], F32)
         nc.gpsimd.memset(ones_f32[:], 1.0)
+        identity_bf = const.tile([P, P], BF16)
+        make_identity(nc, identity_bf[:])
+        identity = const.tile([P, P], F32)
+        make_identity(nc, identity[:])
         eps = const.tile([P, 1], F32)
         nc.gpsimd.memset(eps[:], EPS)
+        minus_half = const.tile([P, GROUP_TILES], F32)
+        nc.gpsimd.memset(minus_half[:], -0.5)
         k_terms_in = const.tile([P, PACK, X_PASSES, P], BF16)
         nc.gpsimd.memset(k_terms_in[:], 0.0)
         row_terms_in = []
         for i in range(2):
             row_terms = const.tile([P, GROUP_TILES, P], BF16, name="row_terms_" + str(i))
             nc.gpsimd.memset(row_terms[:], 0.0)
-            nc.vector.memset(row_terms[:, :, ONE_SLOT : ONE_SLOT + 1], 1.0)
+            nc.gpsimd.memset(row_terms[:, :, ONE_SLOT : ONE_SLOT + 1], 1.0)
             row_terms_in.append(row_terms)
+
+        w_codes = const.tile([P, PASSES, D_OUT], U32, align_bytes=64)
+        w_scales = const.tile([P, PASSES, D_OUT], U8, align_bytes=64)
+        w_grouped_of = {}
+
+        def regroup_w(n):
+            block = stage.tile([P, D_OUT, PACK], BF16, name="block", align_bytes=64)
+            regroup(nc.scalar.copy, w_planes[n], block)
+            w_grouped_of[n] = block
+            if n + W_AHEAD < PASSES:
+                load_w(n + W_AHEAD)
+
+        def quantise_w(n):
+            quantise(nc, w_grouped_of[n], w_codes[:, ORDER[n], :], w_scales[:, ORDER[n], :])
 
         sum_bank = flip_psum.tile([P, GROUP_ROWS], F32, name="bank")
         for t in range(PACK):
@@ -140,58 +162,13 @@ def tile_textguidedcamfusion_pa_kernel(tc, pooled, proto, ln_g, ln_b, W, b, out)
                     stop=True,
                 )
         context_k = const.tile([P, PACK, X_PASSES], F32)
-        nc.vector.tensor_scalar_mul(
+        context_sums = const.tile([P, 1], F32)
+        nc.scalar.activation(
             out=context_k[:].rearrange("p t q -> p (t q)"),
-            in0=sum_bank[:, 0 : PACK * X_PASSES],
-            scalar1=1.0 / PROTOS,
-        )
-
-        gain_shift_f32 = const.tile([P, PACK, P], F32)
-        nc.vector.tensor_copy(
-            out=gain_shift_f32[:], in_=gain_shift_rows[:].rearrange("r (p t) -> r t p", t=PACK)
-        )
-        gain_shift_bank = flip_psum.tile([P, GROUP_ROWS], F32, name="bank")
-        for t in range(PACK):
-            nc.tensor.transpose(
-                gain_shift_bank[:, t * P : (t + 1) * P], gain_shift_f32[:, t, :], identity[:]
-            )
-        gain_shift = const.tile([P, PACK, 2 * PASSES], F32)
-        nc.vector.tensor_copy(
-            out=gain_shift[:],
-            in_=gain_shift_bank[:].rearrange("p (t r) -> p t r", t=PACK)[:, :, 0 : 2 * PASSES],
-        )
-
-        context_stats = const.tile([P, 3], F32)
-        nc.vector.memset(context_stats[:, 0:1], float(CHANNELS))
-
-        def sum_everywhere(values, name):
-            bank = flip_psum.tile([P, GROUP_ROWS], F32, name="bank")
-            nc.tensor.matmul(
-                bank[:, 0 : PACK * X_PASSES],
-                lhsT=ones_f32[:],
-                rhs=values[:].rearrange("p t q -> p (t q)"),
-                start=True,
-                stop=True,
-            )
-            total = const.tile([P, 1], F32, name=name)
-            nc.vector.tensor_reduce(out=total[:], in_=bank[:, 0 : PACK * X_PASSES], op=ALU.add, axis=AXIS.X)
-            return total
-
-        context_sum = sum_everywhere(context_k, "context_sum")
-        nc.vector.tensor_scalar_mul(out=context_stats[:, 1:2], in0=context_sum[:], scalar1=1.0 / CHANNELS)
-        centred = const.tile([P, PACK, X_PASSES], F32)
-        nc.vector.tensor_scalar(
-            out=centred[:], in0=context_k[:], scalar1=context_stats[:, 1:2], scalar2=None, op0=ALU.subtract
-        )
-        nc.vector.tensor_tensor(out=centred[:], in0=centred[:], in1=centred[:], op=ALU.mult)
-        squared_sum = sum_everywhere(centred, "squared_sum")
-        nc.vector.tensor_copy(out=context_stats[:, 2:3], in_=squared_sum[:])
-
-        own = 6 * STATS_PER_TILE
-        stats = const.tile([P, ROW_TILES, own + 3], F32)
-        nc.vector.tensor_copy(
-            out=stats[:, :, own : own + 3],
-            in_=context_stats[:].unsqueeze(1).to_broadcast([P, ROW_TILES, 3]),
+            in_=sum_bank[:, 0 : PACK * X_PASSES],
+            func=ACT.Copy,
+            scale=1.0 / PROTOS,
+            accum_out=context_sums[:],
         )
 
         context_row = const.tile([P, K_PASS], F32)
@@ -206,19 +183,56 @@ def tile_textguidedcamfusion_pa_kernel(tc, pooled, proto, ln_g, ln_b, W, b, out)
             scale=1.0 / PROTOS,
         )
 
+        context_stats = const.tile([P, 3], F32)
+        nc.gpsimd.memset(context_stats[:, 0:1], float(CHANNELS))
+        mean_bank = flip_psum.tile([P, GROUP_ROWS], F32, name="bank")
+        nc.tensor.matmul(mean_bank[:, 0:1], lhsT=ones_f32[:], rhs=context_sums[:], start=True, stop=True)
+        minus_mean = const.tile([P, 1], F32)
+        nc.scalar.activation(
+            out=context_stats[:, 1:2], in_=mean_bank[:, 0:1], func=ACT.Copy, scale=1.0 / CHANNELS
+        )
+        nc.scalar.activation(out=minus_mean[:], in_=mean_bank[:, 0:1], func=ACT.Copy, scale=-1.0 / CHANNELS)
+        centred = const.tile([P, PACK * X_PASSES], F32)
+        squared_sums = const.tile([P, 1], F32)
+        nc.scalar.activation(
+            out=centred[:],
+            in_=context_k[:].rearrange("p t q -> p (t q)"),
+            func=ACT.Square,
+            bias=minus_mean[:],
+            accum_out=squared_sums[:],
+        )
+        square_bank = flip_psum.tile([P, GROUP_ROWS], F32, name="bank")
+        nc.tensor.matmul(square_bank[:, 0:1], lhsT=ones_f32[:], rhs=squared_sums[:], start=True, stop=True)
+        nc.scalar.copy(out=context_stats[:, 2:3], in_=square_bank[:, 0:1])
+
+        own = 6 * STATS_PER_TILE
+        stats = const.tile([P, ROW_TILES, own + 3], F32)
+        nc.vector.tensor_copy(
+            out=stats[:, :, own : own + 3],
+            in_=context_stats[:].unsqueeze(1).to_broadcast([P, ROW_TILES, 3]),
+        )
+
+        gain_shift_bank = flip_psum.tile([P, PACK, P], BF16, name="bank")
+        for t in range(PACK):
+            nc.tensor.transpose(gain_shift_bank[:, t, :], gain_shift_rows[:, t::PACK], identity_bf[:])
+        gain_shift = const.tile([P, PACK, 2 * PASSES], F32)
+        nc.scalar.copy(out=gain_shift[:], in_=gain_shift_bank[:, :, 0 : 2 * PASSES])
+        for n in range(W_EARLY):
+            regroup_w(n)
+
         k_pieces = const.tile([P, PACK, X_PASSES, SLOTS], BF16)
         rest = const.tile([P, PACK, X_PASSES], F32)
-        nc.vector.tensor_tensor(
+        nc.gpsimd.tensor_tensor(
             out=rest[:], in0=context_k[:], in1=gain_shift[:, :, X_PASSES:PASSES], op=ALU.mult
         )
         for u in range(PIECES):
-            nc.vector.tensor_copy(out=k_pieces[:, :, :, u], in_=rest[:])
+            nc.gpsimd.tensor_copy(out=k_pieces[:, :, :, u], in_=rest[:])
             if u + 1 < PIECES:
-                nc.vector.tensor_tensor(out=rest[:], in0=rest[:], in1=k_pieces[:, :, :, u], op=ALU.subtract)
-        nc.vector.tensor_copy(out=k_pieces[:, :, :, PIECES], in_=gain_shift[:, :, X_PASSES:PASSES])
+                nc.gpsimd.tensor_tensor(out=rest[:], in0=rest[:], in1=k_pieces[:, :, :, u], op=ALU.subtract)
+        nc.gpsimd.tensor_copy(out=k_pieces[:, :, :, PIECES], in_=gain_shift[:, :, X_PASSES:PASSES])
         for j in range(PIECES):
-            nc.vector.tensor_copy(out=k_terms_in[:, :, :, j * SLOTS : (j + 1) * SLOTS], in_=k_pieces[:])
-        nc.vector.tensor_copy(
+            nc.gpsimd.tensor_copy(out=k_terms_in[:, :, :, j * SLOTS : (j + 1) * SLOTS], in_=k_pieces[:])
+        nc.gpsimd.tensor_copy(
             out=k_terms_in[:, :, :, ONE_SLOT], in_=gain_shift[:, :, PASSES + X_PASSES : 2 * PASSES]
         )
         k_terms = const.tile([P, OUTER_PASSES, PACK, P], BF16)
@@ -227,16 +241,6 @@ def tile_textguidedcamfusion_pa_kernel(tc, pooled, proto, ln_g, ln_b, W, b, out)
             for t in range(PACK):
                 nc.tensor.transpose(bank[:, t, :], k_terms_in[:, t, q, :], identity_bf[:])
             nc.scalar.copy(out=k_terms[:, q, :, :], in_=bank[:])
-
-        w_codes = const.tile([P, PASSES, D_OUT], U32, align_bytes=64)
-        w_scales = const.tile([P, PASSES, D_OUT], U8, align_bytes=64)
-
-        def quantise_w(n):
-            w_grouped = w_stage.tile([P, D_OUT, PACK], BF16, align_bytes=64, name="w_grouped")
-            regroup(nc.scalar.copy, w_planes[n], w_grouped)
-            quantise(nc, w_grouped, w_codes[:, ORDER[n], :], w_scales[:, ORDER[n], :])
-            if n + W_AHEAD < PASSES:
-                load_w(n + W_AHEAD)
 
         def tile_statistics(rt, j):
             cols = slice(j * STAT_WIDTH, (j + 1) * STAT_WIDTH)
@@ -272,10 +276,10 @@ def tile_textguidedcamfusion_pa_kernel(tc, pooled, proto, ln_g, ln_b, W, b, out)
             left = row_scale[s]
             for j in range(PIECES):
                 piece = terms[:, :, j * SLOTS : (j + 1) * SLOTS]
-                nc.vector.tensor_copy(out=piece, in_=left[:])
+                nc.gpsimd.tensor_copy(out=piece, in_=left[:])
                 if j + 1 < PIECES:
                     rest_of_rows = small.tile([P, GROUP_TILES, SLOTS], F32, name="rest_of_rows")
-                    nc.vector.tensor_tensor(out=rest_of_rows[:], in0=left[:], in1=piece, op=ALU.subtract)
+                    nc.gpsimd.tensor_tensor(out=rest_of_rows[:], in0=left[:], in1=piece, op=ALU.subtract)
                     left = rest_of_rows
 
         def flip_rows(s):
@@ -296,7 +300,7 @@ def tile_textguidedcamfusion_pa_kernel(tc, pooled, proto, ln_g, ln_b, W, b, out)
                 "p (h w t) -> p h t w", t=PACK, w=P
             )
             target = y_slabs[(s, slab)][:, r, :].rearrange("p (h t w) -> p h t w", t=PACK, w=P)
-            if r < GROUP_TILES - 1:
+            if r < VECTOR_TILES:
                 nc.vector.tensor_scalar(
                     out=target,
                     in0=source,
@@ -426,9 +430,8 @@ def tile_textguidedcamfusion_pa_kernel(tc, pooled, proto, ln_g, ln_b, W, b, out)
 
         def norms(s):
             inverse_norm = small.tile([P, GROUP_TILES], F32, name="inverse_norm")
-            nc.scalar.activation(out=inverse_norm[:], in_=square_sums[s][:], func=ACT.Sqrt)
-            nc.vector.tensor_scalar_max(out=inverse_norm[:], in0=inverse_norm[:], scalar1=TINY_NORM)
-            nc.vector.reciprocal(out=inverse_norm[:], in_=inverse_norm[:])
+            nc.gpsimd.tensor_scalar_max(out=inverse_norm[:], in0=square_sums[s][:], scalar1=TINY_NORM**2)
+            nc.gpsimd.tensor_tensor(out=inverse_norm[:], in0=inverse_norm[:], in1=minus_half[:], op=ALU.pow)
             inverse_norms[s] = inverse_norm
 
         def scale_and_store(s, r):
@@ -450,13 +453,21 @@ def tile_textguidedcamfusion_pa_kernel(tc, pooled, proto, ln_g, ln_b, W, b, out)
         def at(step, call, *arguments):
             jobs.setdefault(step, []).append((call, arguments))
 
+        for n in range(W_EARLY, PASSES):
+            at(n - W_EARLY, regroup_w, n)
+        for n in range(1, PASSES):
+            at(n - 1, quantise_w, n)
+        at(1, load_group, 2)
+        at(4, load_group, 3)
+        at(5, nc.scalar.dma_start, bias_rows[:], b.partition_broadcast(P))
         for s in range(GROUPS):
             start = s * PASSES
             for r in all_tiles:
                 if s > 0:
                     at(start - 4 + r, normalise_pooled, s, 0, r)
                 at(start + r, normalise_pooled, s, 1, r)
-                at(start + 2 + r, normalise_context, s, r)
+                if s > 0 or r > 0:
+                    at(start - 1 + r, normalise_context, s, r)
             if s > 0:
                 stat_steps = 4 if s == 1 else 8
                 parts = [(rt, j) for rt in range(s * 4, s * 4 + 4) for j in range(STATS_PER_TILE)]
@@ -482,6 +493,8 @@ def tile_textguidedcamfusion_pa_kernel(tc, pooled, proto, ln_g, ln_b, W, b, out)
             normalise_pooled(0, 0, r)
         split_rows(0)
         flip_rows(0)
+        normalise_context(0, 0)
+        quantise_w(0)
 
         z_planes_of = {}
         z_grouped_of = {}
@@ -498,8 +511,6 @@ def tile_textguidedcamfusion_pa_kernel(tc, pooled, proto, ln_g, ln_b, W, b, out)
                     z_grouped_of[step] = outer(s, g)
                 else:
                     z_planes_of[step] = flip(s, g)
-                if s == 0:
-                    quantise_w(n)
             if step - REGROUP_LAG in z_planes_of:
                 z_grouped_of[step - REGROUP_LAG] = regroup_z(z_planes_of[step - REGROUP_LAG])
             if 0 <= step - QUANTISE_LAG < TOTAL_PASSES:

@@ -34,7 +34,7 @@ STAT_WIDTH = 512
 STATS_PER_TILE = CHANNELS // STAT_WIDTH
 SLAB = 1024
 SLAB_PASSES = SLAB // K_PASS
-VECTOR_TILES = 2
+VECTOR_TILES = 3
 PIECES = 3
 SLOTS = 4
 ONE_SLOT = PIECES * SLOTS
@@ -115,6 +115,8 @@ def tile_textguidedcamfusion_pa_kernel(tc, pooled, proto, ln_g, ln_b, W, b, out)
         )
         bias_rows = const.tile([P, D_OUT], BF16)
 
+        eps = const.tile([P, 1], F32)
+        nc.gpsimd.memset(eps[:], EPS)
         ones = const.tile([P, P], BF16)
         nc.gpsimd.memset(ones[:], 1.0)
         ones_f32 = const.tile([P, P], F32)
@@ -123,17 +125,13 @@ def tile_textguidedcamfusion_pa_kernel(tc, pooled, proto, ln_g, ln_b, W, b, out)
         make_identity(nc, identity_bf[:])
         identity = const.tile([P, P], F32)
         make_identity(nc, identity[:])
-        eps = const.tile([P, 1], F32)
-        nc.gpsimd.memset(eps[:], EPS)
-        minus_half = const.tile([P, GROUP_TILES], F32)
-        nc.gpsimd.memset(minus_half[:], -0.5)
         k_terms_in = const.tile([P, PACK, X_PASSES, P], BF16)
         nc.gpsimd.memset(k_terms_in[:], 0.0)
         row_terms_in = []
         for i in range(2):
             row_terms = const.tile([P, GROUP_TILES, P], BF16, name="row_terms_" + str(i))
             nc.gpsimd.memset(row_terms[:], 0.0)
-            nc.gpsimd.memset(row_terms[:, :, ONE_SLOT : ONE_SLOT + 1], 1.0)
+            nc.vector.memset(row_terms[:, :, ONE_SLOT : ONE_SLOT + 1], 1.0)
             row_terms_in.append(row_terms)
 
         w_codes = const.tile([P, PASSES, D_OUT], U32, align_bytes=64)
@@ -149,6 +147,9 @@ def tile_textguidedcamfusion_pa_kernel(tc, pooled, proto, ln_g, ln_b, W, b, out)
 
         def quantise_w(n):
             quantise(nc, w_grouped_of[n], w_codes[:, ORDER[n], :], w_scales[:, ORDER[n], :])
+
+        warm = const.tile([P, 1], F32)
+        nc.scalar.activation(out=warm[:], in_=eps[:], func=ACT.Sqrt)
 
         sum_bank = flip_psum.tile([P, GROUP_ROWS], F32, name="bank")
         for t in range(PACK):
@@ -276,10 +277,10 @@ def tile_textguidedcamfusion_pa_kernel(tc, pooled, proto, ln_g, ln_b, W, b, out)
             left = row_scale[s]
             for j in range(PIECES):
                 piece = terms[:, :, j * SLOTS : (j + 1) * SLOTS]
-                nc.gpsimd.tensor_copy(out=piece, in_=left[:])
+                nc.vector.tensor_copy(out=piece, in_=left[:])
                 if j + 1 < PIECES:
                     rest_of_rows = small.tile([P, GROUP_TILES, SLOTS], F32, name="rest_of_rows")
-                    nc.gpsimd.tensor_tensor(out=rest_of_rows[:], in0=left[:], in1=piece, op=ALU.subtract)
+                    nc.vector.tensor_tensor(out=rest_of_rows[:], in0=left[:], in1=piece, op=ALU.subtract)
                     left = rest_of_rows
 
         def flip_rows(s):
@@ -405,14 +406,15 @@ def tile_textguidedcamfusion_pa_kernel(tc, pooled, proto, ln_g, ln_b, W, b, out)
 
         hs_of = {}
         square_sums = {}
+        last_sums = const.tile([P, 2], F32)
         inverse_norms = {}
 
         def add_bias(s):
-            hs_of[s] = []
-            for r in range(GROUP_TILES):
+            hs_of[s] = {}
+            for r in (2, 3, 0, 1):
                 h = tail.tile([P, D_OUT], F32, name="h", bufs=2 * GROUP_TILES)
                 nc.vector.tensor_tensor(out=h[:], in0=accs_of[s][r][:], in1=bias_rows[:], op=ALU.add)
-                hs_of[s].append(h)
+                hs_of[s][r] = h
 
         def square(s, r):
             if r == 0:
@@ -428,10 +430,23 @@ def tile_textguidedcamfusion_pa_kernel(tc, pooled, proto, ln_g, ln_b, W, b, out)
                 accum_out=square_sums[s][:, r : r + 1],
             )
 
+        def square_on_scalar(s, r):
+            h = hs_of[s][r]
+            nc.scalar.activation(out=h[:], in_=h[:], func=ACT.Relu)
+            squares = tail.tile([P, D_OUT], F32, name="squares_on_scalar", bufs=1)
+            nc.scalar.activation(
+                out=squares[:], in_=h[:], func=ACT.Square, accum_out=last_sums[:, r - 2 : r - 1]
+            )
+
         def norms(s):
             inverse_norm = small.tile([P, GROUP_TILES], F32, name="inverse_norm")
-            nc.gpsimd.tensor_scalar_max(out=inverse_norm[:], in0=square_sums[s][:], scalar1=TINY_NORM**2)
-            nc.gpsimd.tensor_tensor(out=inverse_norm[:], in0=inverse_norm[:], in1=minus_half[:], op=ALU.pow)
+            if s + 1 < GROUPS:
+                nc.scalar.activation(out=inverse_norm[:], in_=square_sums[s][:], func=ACT.Sqrt)
+            else:
+                nc.scalar.activation(out=inverse_norm[:, 2:4], in_=last_sums[:], func=ACT.Sqrt)
+                nc.scalar.activation(out=inverse_norm[:, 0:2], in_=square_sums[s][:, 0:2], func=ACT.Sqrt)
+            nc.vector.tensor_scalar_max(out=inverse_norm[:], in0=inverse_norm[:], scalar1=TINY_NORM)
+            nc.vector.reciprocal(out=inverse_norm[:], in_=inverse_norm[:])
             inverse_norms[s] = inverse_norm
 
         def scale_and_store(s, r):
@@ -445,6 +460,12 @@ def tile_textguidedcamfusion_pa_kernel(tc, pooled, proto, ln_g, ln_b, W, b, out)
                 op0=ALU.max,
                 op1=ALU.mult,
             )
+            nc.sync.dma_start(out=out[rt * P : (rt + 1) * P, :], in_=h[:])
+
+        def scale_on_scalar(s, r):
+            rt = s * GROUP_TILES + r
+            h = hs_of[s][r]
+            nc.scalar.activation(out=h[:], in_=h[:], func=ACT.Copy, scale=inverse_norms[s][:, r : r + 1])
             nc.sync.dma_start(out=out[rt * P : (rt + 1) * P, :], in_=h[:])
 
         all_tiles = range(GROUP_TILES)
@@ -478,12 +499,21 @@ def tile_textguidedcamfusion_pa_kernel(tc, pooled, proto, ln_g, ln_b, W, b, out)
                 at(start - 2, flip_rows, s)
             done = start + PASSES - 1 + MULTIPLY_LAG
             at(done, add_bias, s)
-            apart = 1 if s + 1 < GROUPS else 0
-            for r in all_tiles:
-                at(done + 1 + apart * r, square, s, r)
-            at(done + 1 + apart * 4, norms, s)
-            for r in all_tiles:
-                at(done + 1 + apart * (5 + r), scale_and_store, s, r)
+            if s + 1 < GROUPS:
+                for r in all_tiles:
+                    at(done + 1 + r, square, s, r)
+                at(done + 5, norms, s)
+                for r in all_tiles:
+                    at(done + 6 + r, scale_and_store, s, r)
+            else:
+                for r in (2, 3):
+                    at(done, square_on_scalar, s, r)
+                for r in (0, 1):
+                    at(done, square, s, r)
+                at(done, norms, s)
+                for r in (0, 1):
+                    at(done, scale_and_store, s, r)
+                    at(done, scale_on_scalar, s, r + 2)
 
         for r in all_tiles:
             for j in range(STATS_PER_TILE):

@@ -34,7 +34,6 @@ STAT_WIDTH = 512
 STATS_PER_TILE = CHANNELS // STAT_WIDTH
 SLAB = 1024
 SLAB_PASSES = SLAB // K_PASS
-VECTOR_TILES = 3
 PIECES = 3
 SLOTS = 4
 ONE_SLOT = PIECES * SLOTS
@@ -301,23 +300,14 @@ def tile_textguidedcamfusion_pa_kernel(tc, pooled, proto, ln_g, ln_b, W, b, out)
                 "p (h w t) -> p h t w", t=PACK, w=P
             )
             target = y_slabs[(s, slab)][:, r, :].rearrange("p (h t w) -> p h t w", t=PACK, w=P)
-            if r < VECTOR_TILES:
-                nc.vector.tensor_scalar(
-                    out=target,
-                    in0=source,
-                    scalar1=scale[:, r, 0:1],
-                    scalar2=scale[:, r, PIECES : PIECES + 1],
-                    op0=ALU.mult,
-                    op1=ALU.add,
-                )
-            else:
-                nc.scalar.activation(
-                    out=target,
-                    in_=source,
-                    func=ACT.Identity,
-                    scale=scale[:, r, 0:1],
-                    bias=scale[:, r, PIECES : PIECES + 1],
-                )
+            nc.vector.tensor_scalar(
+                out=target,
+                in0=source,
+                scalar1=scale[:, r, 0:1],
+                scalar2=scale[:, r, PIECES : PIECES + 1],
+                op0=ALU.mult,
+                op1=ALU.add,
+            )
 
         def normalise_context(s, r):
             if r == 0:

@@ -15,6 +15,7 @@ AXIS = mybir.AxisListType
 P = 128
 PACK = 4
 K_PASS = P * PACK
+RUN = 4
 ROWS = 2048
 CHANNELS = 2048
 PROTOS = 64
@@ -78,7 +79,8 @@ def tile_textguidedcamfusion_pa_kernel(tc, pooled, proto, ln_g, ln_b, W, b, out)
 
         x_tiles = {}
         w_planes = {}
-        w_view = W.rearrange("(g p t) n -> g p t n", t=PACK, p=P)
+        w_context = W.rearrange("(g p t) n -> g p t n", t=PACK, p=P)
+        w_pooled = W.rearrange("(g a t b) n -> g t a b n", t=PACK, b=RUN, a=P // RUN)
 
         def load_x(rt):
             block = stage.tile([P, CHANNELS], BF16, name="block", align_bytes=64)
@@ -87,7 +89,12 @@ def tile_textguidedcamfusion_pa_kernel(tc, pooled, proto, ln_g, ln_b, W, b, out)
 
         def load_w(n):
             block = stage.tile([P, PACK, D_OUT], BF16, name="block", align_bytes=64)
-            nc.sync.dma_start(out=block[:], in_=w_view[ORDER[n]])
+            g = ORDER[n]
+            if g < X_PASSES:
+                for t in range(PACK):
+                    nc.sync.dma_start(out=block[:, t, :], in_=w_pooled[g, t])
+            else:
+                nc.sync.dma_start(out=block[:], in_=w_context[g])
             w_planes[n] = block
 
         def load_group(s):
@@ -212,11 +219,24 @@ def tile_textguidedcamfusion_pa_kernel(tc, pooled, proto, ln_g, ln_b, W, b, out)
             in_=context_stats[:].unsqueeze(1).to_broadcast([P, ROW_TILES, 3]),
         )
 
-        gain_shift_bank = flip_psum.tile([P, PACK, P], BF16, name="bank")
-        for t in range(PACK):
-            nc.tensor.transpose(gain_shift_bank[:, t, :], gain_shift_rows[:, t::PACK], identity_bf[:])
+        pooled_rows = const.tile([P, PACK, P], BF16)
+        nc.scalar.copy(
+            out=pooled_rows[:].rearrange("r t (a b) -> r t a b", b=RUN),
+            in_=gain_shift_rows[:].rearrange("r (a t b) -> r t a b", t=PACK, b=RUN),
+        )
         gain_shift = const.tile([P, PACK, 2 * PASSES], F32)
-        nc.scalar.copy(out=gain_shift[:], in_=gain_shift_bank[:, :, 0 : 2 * PASSES])
+        halves = gain_shift[:].rearrange("p t (v g) -> p t v g", v=2)
+        for first in (0, X_PASSES):
+            bank = flip_psum.tile([P, PACK, P], BF16, name="bank")
+            for t in range(PACK):
+                source = pooled_rows[:, t, :] if first == 0 else gain_shift_rows[:, t::PACK]
+                nc.tensor.transpose(bank[:, t, :], source, identity_bf[:])
+            nc.scalar.copy(
+                out=halves[:, :, :, first : first + X_PASSES],
+                in_=bank[:, :, 0 : 2 * PASSES].rearrange("p t (v g) -> p t v g", v=2)[
+                    :, :, :, first : first + X_PASSES
+                ],
+            )
         for n in range(W_EARLY):
             regroup_w(n)
 
@@ -297,9 +317,9 @@ def tile_textguidedcamfusion_pa_kernel(tc, pooled, proto, ln_g, ln_b, W, b, out)
                 y_slabs[(s, slab)] = y_pool.tile([P, GROUP_TILES, SLAB], F32, name="y")
             scale = row_scale[s]
             source = x_tiles[s * GROUP_TILES + r][:, slab * SLAB : (slab + 1) * SLAB].rearrange(
-                "p (h w t) -> p h t w", t=PACK, w=P
+                "p (c t b) -> p t c b", t=PACK, b=RUN
             )
-            target = y_slabs[(s, slab)][:, r, :].rearrange("p (h t w) -> p h t w", t=PACK, w=P)
+            target = y_slabs[(s, slab)][:, r, :].rearrange("p (t c b) -> p t c b", t=PACK, b=RUN)
             nc.vector.tensor_scalar(
                 out=target,
                 in0=source,
@@ -324,17 +344,17 @@ def tile_textguidedcamfusion_pa_kernel(tc, pooled, proto, ln_g, ln_b, W, b, out)
         def flip(s, g):
             if g < X_PASSES:
                 y = y_slabs[(s, g // SLAB_PASSES)]
-                first = (g % SLAB_PASSES) * K_PASS
+                first, apart = (g % SLAB_PASSES) * P, SLAB // PACK
             else:
                 y = y_slabs[(s, PASSES)]
-                first = 0
+                first, apart = 0, P
             z_planes = z_stage.tile([P, PACK, GROUP_ROWS], BF16, name="z_planes")
             for t in range(PACK):
                 bank = flip_psum.tile([P, GROUP_ROWS], F32, name="bank")
                 for r in range(GROUP_TILES):
                     nc.tensor.transpose(
                         bank[:, r * P : (r + 1) * P],
-                        y[:, r, first + t * P : first + (t + 1) * P],
+                        y[:, r, first + t * apart : first + t * apart + P],
                         identity[:],
                     )
                 nc.scalar.activation(

from contextlib import ExitStack

import concourse.mybir as mybir
from concourse.masks import make_identity

F32 = mybir.dt.float32
BF16 = mybir.dt.bfloat16
U32 = mybir.dt.uint32
U8 = mybir.dt.uint8
FP8X4 = mybir.dt.float8_e4m3fn_x4
ACT = mybir.ActivationFunctionType
ALU = mybir.AluOpType
AXIS = mybir.AxisListType

P = 128
PACK = 4
K_PASS = P * PACK
RUN = 4
ROWS = 2048
CHANNELS = 2048
PROTOS = 64
FUSED = 2 * CHANNELS
D_OUT = 512
EPS = 1e-5
TINY_NORM = 1e-12

PASSES = FUSED // K_PASS
X_PASSES = CHANNELS // K_PASS
OUTER_PASSES = 3
GROUP_TILES = 4
GROUP_ROWS = GROUP_TILES * P
GROUPS = ROWS // GROUP_ROWS
ROW_TILES = ROWS // P
STAT_WIDTH = 512
STATS_PER_TILE = CHANNELS // STAT_WIDTH
SLAB = 1024
SLAB_PASSES = SLAB // K_PASS
PIECES = 3
SLOTS = 4
ONE_SLOT = PIECES * SLOTS
TOTAL_PASSES = GROUPS * PASSES
LONG_PASS = PASSES - 1
CONTEXT_ORDER = (X_PASSES, LONG_PASS, X_PASSES + 1, X_PASSES + 2)
ORDER = [g for pair in zip(range(X_PASSES), CONTEXT_ORDER) for g in pair]
REGROUP_LAG = 1
QUANTISE_LAG = 2
MULTIPLY_LAG = 3
W_AHEAD = 5
W_EARLY = 3

FLOPS = 2 * ROWS * FUSED * D_OUT


def regroup(copy, planes, grouped):
    copy(
        out=grouped[:].rearrange("p (c i) t -> p c t i", i=4),
        in_=planes[:].rearrange("p t (c i) -> p c t i", i=4),
    )


def quantise(nc, grouped, codes, scales):
    nc.vector.quantize_mx(
        out=codes.bitcast(FP8X4), scales=scales, in_=grouped[:].rearrange("p w t -> p (w t)")
    )


def tile_textguidedcamfusion_pa_kernel(tc, pooled, proto, ln_g, ln_b, W, b, out):
    nc = tc.nc
    with ExitStack() as stack:
        const = stack.enter_context(tc.tile_pool(name="const", bufs=1))
        stage = stack.enter_context(tc.tile_pool(name="stage", bufs=20))
        y_pool = stack.enter_context(tc.tile_pool(name="y", bufs=2))
        z_stage = stack.enter_context(tc.tile_pool(name="z_stage", bufs=3))
        z_words = stack.enter_context(tc.tile_pool(name="z_words", bufs=3))
        small = stack.enter_context(tc.tile_pool(name="small", bufs=2))
        tail = stack.enter_context(tc.tile_pool(name="tail", bufs=GROUP_TILES))
        flip_psum = stack.enter_context(tc.psum_pool(name="flip_psum", bufs=4))
        acc_psum = stack.enter_context(tc.psum_pool(name="acc_psum", bufs=GROUP_TILES))

        x_tiles = {}
        w_planes = {}
        w_context = W.rearrange("(g p t) n -> g p t n", t=PACK, p=P)
        w_pooled = W.rearrange("(g a t b) n -> g t a b n", t=PACK, b=RUN, a=P // RUN)

        def load_x(rt):
            block = stage.tile([P, CHANNELS], BF16, name="block", align_bytes=64)
            nc.sync.dma_start(out=block[:], in_=pooled[rt * P : (rt + 1) * P, :])
            x_tiles[rt] = block

        def load_w(n):
            block = stage.tile([P, PACK, D_OUT], BF16, name="block", align_bytes=64)
            g = ORDER[n]
            if g < X_PASSES:
                for t in range(PACK):
                    nc.sync.dma_start(out=block[:, t, :], in_=w_pooled[g, t])
            else:
                nc.sync.dma_start(out=block[:], in_=w_context[g])
            w_planes[n] = block

        def load_group(s):
            for rt in range(s * GROUP_TILES, (s + 1) * GROUP_TILES):
                load_x(rt)

        for i in range(2):
            load_x(i)
            load_w(i)
        load_x(2)
        load_x(3)
        for n in range(2, W_AHEAD):
            load_w(n)
        load_group(1)

        proto_rows = const.tile([P, CHANNELS], BF16)
        nc.vector.memset(proto_rows[PROTOS:P, :], 0.0)
        nc.scalar.dma_start(out=proto_rows[0:PROTOS, :], in_=proto)
        gain_shift_rows = const.tile([P, K_PASS], BF16)
        nc.gpsimd.memset(gain_shift_rows[:], 0.0)
        nc.scalar.dma_start(out=gain_shift_rows[0:PASSES, :], in_=ln_g.rearrange("(g k) -> g k", k=K_PASS))
        nc.scalar.dma_start(
            out=gain_shift_rows[PASSES : 2 * PASSES, :], in_=ln_b.rearrange("(g k) -> g k", k=K_PASS)
        )
        bias_rows = const.tile([P, D_OUT], BF16)

        eps = const.tile([P, 1], F32)
        nc.gpsimd.memset(eps[:], EPS)
        ones = const.tile([P, P], BF16)
        nc.gpsimd.memset(ones[:], 1.0)
        ones_f32 = const.tile([P, P], F32)
        nc.gpsimd.memset(ones_f32[:], 1.0)
        identity_bf = const.tile([P, P], BF16)
        make_identity(nc, identity_bf[:])
        identity = const.tile([P, P], F32)
        make_identity(nc, identity[:])
        k_terms_in = const.tile([P, PACK, X_PASSES, P], BF16)
        nc.gpsimd.memset(k_terms_in[:], 0.0)
        row_terms_in = []
        for i in range(2):
            row_terms = const.tile([P, GROUP_TILES, P], BF16, name="row_terms_" + str(i))
            nc.gpsimd.memset(row_terms[:], 0.0)
            nc.vector.memset(row_terms[:, :, ONE_SLOT : ONE_SLOT + 1], 1.0)
            row_terms_in.append(row_terms)

        w_codes = const.tile([P, PASSES, D_OUT], U32, align_bytes=64)
        w_scales = const.tile([P, PASSES, D_OUT], U8, align_bytes=64)
        w_grouped_of = {}

        def regroup_w(n):
            block = stage.tile([P, D_OUT, PACK], BF16, name="block", align_bytes=64)
            regroup(nc.scalar.copy, w_planes[n], block)
            w_grouped_of[n] = block
            if n + W_AHEAD < PASSES:
                load_w(n + W_AHEAD)

        def quantise_w(n):
            quantise(nc, w_grouped_of[n], w_codes[:, ORDER[n], :], w_scales[:, ORDER[n], :])

        warm = const.tile([P, 1], F32)
        nc.scalar.activation(out=warm[:], in_=eps[:], func=ACT.Sqrt)

        sum_bank = flip_psum.tile([P, GROUP_ROWS], F32, name="bank")
        for t in range(PACK):
            for q in range(X_PASSES):
                n = t * X_PASSES + q
                nc.tensor.matmul(
                    sum_bank[:, n : n + 1],
                    lhsT=proto_rows[:, q * K_PASS + t : (q + 1) * K_PASS : PACK],
                    rhs=ones[:, 0:1],
                    start=True,
                    stop=True,
                )
        context_k = const.tile([P, PACK, X_PASSES], F32)
        context_sums = const.tile([P, 1], F32)
        nc.scalar.activation(
            out=context_k[:].rearrange("p t q -> p (t q)"),
            in_=sum_bank[:, 0 : PACK * X_PASSES],
            func=ACT.Copy,
            scale=1.0 / PROTOS,
            accum_out=context_sums[:],
        )

        context_row = const.tile([P, K_PASS], F32)
        row_bank = flip_psum.tile([P, GROUP_ROWS], F32, name="bank")
        nc.tensor.matmul(
            row_bank[:], lhsT=ones[:], rhs=proto_rows[:, OUTER_PASSES * K_PASS :], start=True, stop=True
        )
        nc.scalar.activation(
            out=context_row[:].rearrange("p (t w) -> p t w", t=PACK),
            in_=row_bank[:].rearrange("p (w t) -> p t w", t=PACK),
            func=ACT.Copy,
            scale=1.0 / PROTOS,
        )

        context_stats = const.tile([P, 3], F32)
        nc.gpsimd.memset(context_stats[:, 0:1], float(CHANNELS))
        mean_bank = flip_psum.tile([P, GROUP_ROWS], F32, name="bank")
        nc.tensor.matmul(mean_bank[:, 0:1], lhsT=ones_f32[:], rhs=context_sums[:], start=True, stop=True)
        minus_mean = const.tile([P, 1], F32)
        nc.scalar.activation(
            out=context_stats[:, 1:2], in_=mean_bank[:, 0:1], func=ACT.Copy, scale=1.0 / CHANNELS
        )
        nc.scalar.activation(out=minus_mean[:], in_=mean_bank[:, 0:1], func=ACT.Copy, scale=-1.0 / CHANNELS)
        centred = const.tile([P, PACK * X_PASSES], F32)
        squared_sums = const.tile([P, 1], F32)
        nc.scalar.activation(
            out=centred[:],
            in_=context_k[:].rearrange("p t q -> p (t q)"),
            func=ACT.Square,
            bias=minus_mean[:],
            accum_out=squared_sums[:],
        )
        square_bank = flip_psum.tile([P, GROUP_ROWS], F32, name="bank")
        nc.tensor.matmul(square_bank[:, 0:1], lhsT=ones_f32[:], rhs=squared_sums[:], start=True, stop=True)
        nc.scalar.copy(out=context_stats[:, 2:3], in_=square_bank[:, 0:1])

        own = 6 * STATS_PER_TILE
        stats = const.tile([P, ROW_TILES, own + 3], F32)
        nc.vector.tensor_copy(
            out=stats[:, :, own : own + 3],
            in_=context_stats[:].unsqueeze(1).to_broadcast([P, ROW_TILES, 3]),
        )

        pooled_rows = const.tile([P, PACK, P], BF16)
        nc.scalar.copy(
            out=pooled_rows[:].rearrange("r t (a b) -> r t a b", b=RUN),
            in_=gain_shift_rows[:].rearrange("r (a t b) -> r t a b", t=PACK, b=RUN),
        )
        gain_shift = const.tile([P, PACK, 2 * PASSES], F32)
        halves = gain_shift[:].rearrange("p t (v g) -> p t v g", v=2)
        for first in (0, X_PASSES):
            bank = flip_psum.tile([P, PACK, P], BF16, name="bank")
            for t in range(PACK):
                source = pooled_rows[:, t, :] if first == 0 else gain_shift_rows[:, t::PACK]
                nc.tensor.transpose(bank[:, t, :], source, identity_bf[:])
            nc.scalar.copy(
                out=halves[:, :, :, first : first + X_PASSES],
                in_=bank[:, :, 0 : 2 * PASSES].rearrange("p t (v g) -> p t v g", v=2)[
                    :, :, :, first : first + X_PASSES
                ],
            )
        for n in range(W_EARLY):
            regroup_w(n)

        k_pieces = const.tile([P, PACK, X_PASSES, SLOTS], BF16)
        rest = const.tile([P, PACK, X_PASSES], F32)
        nc.gpsimd.tensor_tensor(
            out=rest[:], in0=context_k[:], in1=gain_shift[:, :, X_PASSES:PASSES], op=ALU.mult
        )
        for u in range(PIECES):
            nc.gpsimd.tensor_copy(out=k_pieces[:, :, :, u], in_=rest[:])
            if u + 1 < PIECES:
                nc.gpsimd.tensor_tensor(out=rest[:], in0=rest[:], in1=k_pieces[:, :, :, u], op=ALU.subtract)
        nc.gpsimd.tensor_copy(out=k_pieces[:, :, :, PIECES], in_=gain_shift[:, :, X_PASSES:PASSES])
        for j in range(PIECES):
            nc.gpsimd.tensor_copy(out=k_terms_in[:, :, :, j * SLOTS : (j + 1) * SLOTS], in_=k_pieces[:])
        nc.gpsimd.tensor_copy(
            out=k_terms_in[:, :, :, ONE_SLOT], in_=gain_shift[:, :, PASSES + X_PASSES : 2 * PASSES]
        )
        k_terms = const.tile([P, OUTER_PASSES, PACK, P], BF16)
        for q in range(OUTER_PASSES):
            bank = flip_psum.tile([P, PACK, P], BF16, name="bank")
            for t in range(PACK):
                nc.tensor.transpose(bank[:, t, :], k_terms_in[:, t, q, :], identity_bf[:])
            nc.scalar.copy(out=k_terms[:, q, :, :], in_=bank[:])

        def tile_statistics(rt, j):
            cols = slice(j * STAT_WIDTH, (j + 1) * STAT_WIDTH)
            nc.vector.bn_stats(out=stats[:, rt, 6 * j : 6 * (j + 1)], in_=x_tiles[rt][:, cols])

        row_scale = {}

        def group_scales(s):
            mean_var = small.tile([P, GROUP_TILES, 2], F32, name="mean_var")
            for r in range(GROUP_TILES):
                nc.vector.bn_aggr(out=mean_var[:, r, :], in_=stats[:, s * GROUP_TILES + r, :])
            std = small.tile([P, GROUP_TILES], F32, name="std")
            nc.scalar.activation(out=std[:], in_=mean_var[:, :, 1], func=ACT.Sqrt, bias=eps[:])
            scale = small.tile([P, GROUP_TILES, SLOTS], F32, name="scale")
            nc.vector.reciprocal(
                out=scale[:, :, 0:PIECES],
                in_=std[:].unsqueeze(2).to_broadcast([P, GROUP_TILES, PIECES]),
            )
            nc.vector.scalar_tensor_tensor(
                out=scale[:, :, PIECES],
                in0=mean_var[:, :, 0],
                scalar=-1.0,
                in1=scale[:, :, 0],
                op0=ALU.mult,
                op1=ALU.mult,
            )
            row_scale[s] = scale

        row_terms_of = {}

        def split_rows(s):
            terms = row_terms_in[s % 2]
            left = row_scale[s]
            for j in range(PIECES):
                piece = terms[:, :, j * SLOTS : (j + 1) * SLOTS]
                nc.vector.tensor_copy(out=piece, in_=left[:])
                if j + 1 < PIECES:
                    rest_of_rows = small.tile([P, GROUP_TILES, SLOTS], F32, name="rest_of_rows")
                    nc.vector.tensor_tensor(out=rest_of_rows[:], in0=left[:], in1=piece, op=ALU.subtract)
                    left = rest_of_rows

        def flip_rows(s):
            bank = flip_psum.tile([P, GROUP_TILES, P], BF16, name="bank")
            for r in range(GROUP_TILES):
                nc.tensor.transpose(bank[:, r, :], row_terms_in[s % 2][:, r, :], identity_bf[:])
            row_terms = small.tile([P, GROUP_ROWS], BF16, name="row_terms")
            nc.scalar.copy(out=row_terms[:], in_=bank[:].rearrange("p r i -> p (r i)"))
            row_terms_of[s] = row_terms

        y_slabs = {}

        def normalise_pooled(s, slab, r):
            if r == 0:
                y_slabs[(s, slab)] = y_pool.tile([P, GROUP_TILES, SLAB], F32, name="y")
            scale = row_scale[s]
            source = x_tiles[s * GROUP_TILES + r][:, slab * SLAB : (slab + 1) * SLAB].rearrange(
                "p (c t b) -> p t c b", t=PACK, b=RUN
            )
            target = y_slabs[(s, slab)][:, r, :].rearrange("p (t c b) -> p t c b", t=PACK, b=RUN)
            nc.vector.tensor_scalar(
                out=target,
                in0=source,
                scalar1=scale[:, r, 0:1],
                scalar2=scale[:, r, PIECES : PIECES + 1],
                op0=ALU.mult,
                op1=ALU.add,
            )

        def normalise_context(s, r):
            if r == 0:
                y_slabs[(s, PASSES)] = y_pool.tile([P, GROUP_TILES, K_PASS], F32, name="y_context", bufs=1)
            scale = row_scale[s]
            nc.scalar.activation(
                out=y_slabs[(s, PASSES)][:, r, :],
                in_=context_row[:],
                func=ACT.Identity,
                scale=scale[:, r, 0:1],
                bias=scale[:, r, PIECES : PIECES + 1],
            )

        def flip(s, g):
            if g < X_PASSES:
                y = y_slabs[(s, g // SLAB_PASSES)]
                first, apart = (g % SLAB_PASSES) * P, SLAB // PACK
            else:
                y = y_slabs[(s, PASSES)]
                first, apart = 0, P
            z_planes = z_stage.tile([P, PACK, GROUP_ROWS], BF16, name="z_planes")
            for t in range(PACK):
                bank = flip_psum.tile([P, GROUP_ROWS], F32, name="bank")
                for r in range(GROUP_TILES):
                    nc.tensor.transpose(
                        bank[:, r * P : (r + 1) * P],
                        y[:, r, first + t * apart : first + t * apart + P],
                        identity[:],
                    )
                nc.scalar.activation(
                    out=z_planes[:, t, :],
                    in_=bank[:],
                    func=ACT.Identity,
                    scale=gain_shift[:, t, g : g + 1],
                    bias=gain_shift[:, t, PASSES + g : PASSES + g + 1],
                )
            return z_planes

        def outer(s, g):
            z_grouped = z_stage.tile([P, GROUP_ROWS, PACK], BF16, align_bytes=64, name="z_grouped")
            half_rows = GROUP_ROWS // 2
            for half in range(2):
                rows = slice(half * half_rows, (half + 1) * half_rows)
                bank = flip_psum.tile([P, PACK, half_rows], BF16, name="bank")
                for t in range(PACK):
                    nc.tensor.matmul(
                        bank[:, t, :],
                        lhsT=k_terms[:, g - X_PASSES, t, :],
                        rhs=row_terms_of[s][:, rows],
                        start=True,
                        stop=True,
                    )
                nc.scalar.copy(out=z_grouped[:, rows, :], in_=bank[:].rearrange("p t i -> p i t"))
            return z_grouped

        def regroup_z(z_planes):
            z_grouped = z_stage.tile([P, GROUP_ROWS, PACK], BF16, align_bytes=64, name="z_grouped")
            regroup(nc.vector.tensor_copy, z_planes, z_grouped)
            return z_grouped

        def quantise_z(z_grouped):
            z_codes = z_words.tile([P, GROUP_ROWS], U32, align_bytes=64, name="z_codes")
            z_scales = z_words.tile([P, GROUP_ROWS], U8, align_bytes=64, name="z_scales")
            quantise(nc, z_grouped, z_codes[:], z_scales[:])
            return z_codes, z_scales

        accs_of = {}

        def multiply(s, n, z_codes, z_scales):
            if n == 0:
                accs_of[s] = []
                for r in range(GROUP_TILES):
                    acc = acc_psum.tile([P, D_OUT], F32, name="acc")
                    accs_of[s].append(acc)
            for r in range(GROUP_TILES):
                rows = slice(r * P, (r + 1) * P)
                nc.tensor.matmul_mx(
                    out=accs_of[s][r][:],
                    lhsT=z_codes[:, rows].bitcast(FP8X4),
                    lhsT_scale=z_scales[:, rows],
                    rhs=w_codes[:, ORDER[n], :].bitcast(FP8X4),
                    rhs_scale=w_scales[:, ORDER[n], :],
                    start=(n == 0),
                    stop=(n == PASSES - 1),
                )

        hs_of = {}
        square_sums = {}
        last_sums = const.tile([P, 2], F32)
        inverse_norms = {}

        def add_bias(s):
            hs_of[s] = {}
            for r in (2, 3, 0, 1):
                h = tail.tile([P, D_OUT], F32, name="h", bufs=2 * GROUP_TILES)
                nc.vector.tensor_tensor(out=h[:], in0=accs_of[s][r][:], in1=bias_rows[:], op=ALU.add)
                hs_of[s][r] = h

        def square(s, r):
            if r == 0:
                square_sums[s] = small.tile([P, GROUP_TILES], F32, name="square_sum")
            squares = tail.tile([P, D_OUT], F32, name="squares", bufs=2)
            nc.vector.scalar_tensor_tensor(
                out=squares[:],
                in0=hs_of[s][r][:],
                scalar=0.0,
                in1=hs_of[s][r][:],
                op0=ALU.max,
                op1=ALU.mult,
                accum_out=square_sums[s][:, r : r + 1],
            )

        def square_on_scalar(s, r):
            h = hs_of[s][r]
            nc.scalar.activation(out=h[:], in_=h[:], func=ACT.Relu)
            squares = tail.tile([P, D_OUT], F32, name="squares_on_scalar", bufs=1)
            nc.scalar.activation(
                out=squares[:], in_=h[:], func=ACT.Square, accum_out=last_sums[:, r - 2 : r - 1]
            )

        def norms(s):
            inverse_norm = small.tile([P, GROUP_TILES], F32, name="inverse_norm")
            if s + 1 < GROUPS:
                nc.scalar.activation(out=inverse_norm[:], in_=square_sums[s][:], func=ACT.Sqrt)
            else:
                nc.scalar.activation(out=inverse_norm[:, 2:4], in_=last_sums[:], func=ACT.Sqrt)
                nc.scalar.activation(out=inverse_norm[:, 0:2], in_=square_sums[s][:, 0:2], func=ACT.Sqrt)
            nc.vector.tensor_scalar_max(out=inverse_norm[:], in0=inverse_norm[:], scalar1=TINY_NORM)
            nc.vector.reciprocal(out=inverse_norm[:], in_=inverse_norm[:])
            inverse_norms[s] = inverse_norm

        def scale_and_store(s, r):
            rt = s * GROUP_TILES + r
            h = hs_of[s][r]
            nc.vector.tensor_scalar(
                out=h[:],
                in0=h[:],
                scalar1=0.0,
                scalar2=inverse_norms[s][:, r : r + 1],
                op0=ALU.max,
                op1=ALU.mult,
            )
            nc.sync.dma_start(out=out[rt * P : (rt + 1) * P, :], in_=h[:])

        def scale_on_scalar(s, r):
            rt = s * GROUP_TILES + r
            h = hs_of[s][r]
            nc.scalar.activation(out=h[:], in_=h[:], func=ACT.Copy, scale=inverse_norms[s][:, r : r + 1])
            nc.sync.dma_start(out=out[rt * P : (rt + 1) * P, :], in_=h[:])

        all_tiles = range(GROUP_TILES)
        jobs = {}

        def at(step, call, *arguments):
            jobs.setdefault(step, []).append((call, arguments))

        for n in range(W_EARLY, PASSES):
            at(n - W_EARLY, regroup_w, n)
        for n in range(1, PASSES):
            at(n - 1, quantise_w, n)
        at(1, load_group, 2)
        at(4, load_group, 3)
        at(5, nc.scalar.dma_start, bias_rows[:], b.partition_broadcast(P))
        for s in range(GROUPS):
            start = s * PASSES
            for r in all_tiles:
                if s > 0:
                    at(start - 4 + r, normalise_pooled, s, 0, r)
                at(start + r, normalise_pooled, s, 1, r)
                if s > 0 or r > 0:
                    at(start - 1 + r, normalise_context, s, r)
            if s > 0:
                stat_steps = 4 if s == 1 else 8
                parts = [(rt, j) for rt in range(s * 4, s * 4 + 4) for j in range(STATS_PER_TILE)]
                for i, (rt, j) in enumerate(parts):
                    at(start - 4 - stat_steps + i * stat_steps // len(parts), tile_statistics, rt, j)
                at(start - 5, group_scales, s)
                at(start - 4, split_rows, s)
                at(start - 2, flip_rows, s)
            done = start + PASSES - 1 + MULTIPLY_LAG
            at(done, add_bias, s)
            if s + 1 < GROUPS:
                for r in all_tiles:
                    at(done + 1 + r, square, s, r)
                at(done + 5, norms, s)
                for r in all_tiles:
                    at(done + 6 + r, scale_and_store, s, r)
            else:
                for r in (2, 3):
                    at(done, square_on_scalar, s, r)
                for r in (0, 1):
                    at(done, square, s, r)
                at(done, norms, s)
                for r in (0, 1):
                    at(done, scale_and_store, s, r)
                    at(done, scale_on_scalar, s, r + 2)

        for r in all_tiles:
            for j in range(STATS_PER_TILE):
                tile_statistics(r, j)
        group_scales(0)
        for r in all_tiles:
            normalise_pooled(0, 0, r)
        split_rows(0)
        flip_rows(0)
        normalise_context(0, 0)
        quantise_w(0)

        z_planes_of = {}
        z_grouped_of = {}
        z_words_of = {}
        for step in range(TOTAL_PASSES + MULTIPLY_LAG + 2):
            multiplied = step - MULTIPLY_LAG
            if 0 <= multiplied < TOTAL_PASSES:
                s, n = divmod(multiplied, PASSES)
                multiply(s, n, *z_words_of[multiplied])
            if step < TOTAL_PASSES:
                s, n = divmod(step, PASSES)
                g = ORDER[n]
                if X_PASSES <= g < X_PASSES + OUTER_PASSES:
                    z_grouped_of[step] = outer(s, g)
                else:
                    z_planes_of[step] = flip(s, g)
            if step - REGROUP_LAG in z_planes_of:
                z_grouped_of[step - REGROUP_LAG] = regroup_z(z_planes_of[step - REGROUP_LAG])
            if 0 <= step - QUANTISE_LAG < TOTAL_PASSES:
                z_words_of[step - QUANTISE_LAG] = quantise_z(z_grouped_of[step - QUANTISE_LAG])
            for call, arguments in jobs.get(step, []):
                call(*arguments)
